import numpy as np
import ml_dtypes


def mxq(x, axis, fmt="e4m3"):
    dtype, down = {"e4m3": (ml_dtypes.float8_e4m3fn, 7), "e5m2": (ml_dtypes.float8_e5m2, 14)}[fmt]
    v = np.moveaxis(np.asarray(x, np.float32).astype(ml_dtypes.bfloat16).astype(np.float64), axis, -1)
    blocks = v.reshape(v.shape[:-1] + (-1, 32))
    amax = np.abs(blocks).max(-1, keepdims=True)
    byte = np.maximum(np.where(amax > 0, np.frexp(amax)[1] - 1 + 127, 0) - down, 1)
    scale = np.exp2(byte - 127.0)
    codes = (blocks / scale).astype(np.float32).astype(dtype).astype(np.float64)
    return np.moveaxis((codes * scale).reshape(v.shape), -1, axis)


WIDE = False


def mx_kscale(k):
    if not WIDE:
        return np.ones(k)
    levels = np.array([10, -10, 5, -5, 0])
    if k % 512:
        return np.exp2(np.random.permutation(np.resize(levels, k // 32))).repeat(32)
    a = np.empty((k // 512, 16))
    for p in range(k // 512):
        a[p, :8] = np.random.permutation(np.resize(levels, 8))
        for g in range(8):
            far = levels[np.abs(levels - a[p, g]) >= 10]
            a[p, g + 8] = far[np.random.randint(len(far))]
    return np.exp2(a.ravel()).repeat(32)


BF16 = ml_dtypes.bfloat16


def bf(x):
    return np.asarray(x, np.float32).astype(BF16)


def f64(x):
    return np.asarray(x).astype(np.float64)


B, N, O, M1, F, H, A = 128, 8, 128, 512, 1024, 256, 16
NG = 4
G = NG * H


def sigmoid(v):
    return 1.0 / (1.0 + np.exp(-v))


def setup_inputs():
    s, t = mx_kscale(M1), mx_kscale(F)
    r = np.random.standard_normal
    return {
        "f_hid": bf(np.maximum(r((B, N, M1)), 0.0) * s),
        "h0": bf(r((N, B, H))),
        "c0": bf(r((N, B, H))),
        "W2": bf(r((F, M1)) * 1.4 / np.sqrt(M1) / s[None, :] * t[:, None]),
        "b2": bf(r(F) * 0.2 * t),
        "W_ih": bf(r((N, G, F)) * 1.4 / np.sqrt(F) / t[None, None, :]),
        "W_hh": bf(r((N, G, H)) / np.sqrt(H)),
        "b_ih": bf(r((N, G)) * 0.2),
        "b_hh": bf(r((N, G)) * 0.2),
    }


def reference(f_hid, h0, c0, W2, b2, W_ih, W_hh, b_ih, b_hh):
    f = np.maximum((mxq(f64(f_hid), 2, "e4m3") @ mxq(f64(W2), 1, "e4m3").T) + f64(b2), 0.0)
    feats = f.transpose(1, 0, 2)
    gates = ((mxq(feats, 2, "e4m3") @ mxq(f64(W_ih), 2, "e4m3").transpose(0, 2, 1)) + f64(b_ih)[:, None, :]
             + f64(h0) @ f64(W_hh).transpose(0, 2, 1) + f64(b_hh)[:, None, :])
    i_g, f_g, g_g, o_g = np.split(gates, NG, axis=-1)
    i_g = sigmoid(i_g)
    f_g = sigmoid(f_g)
    g_g = np.tanh(g_g)
    o_g = sigmoid(o_g)
    c_new = f_g * f64(c0) + i_g * g_g
    h_new = o_g * np.tanh(c_new)
    return h_new, c_new

@@ -1,0 +1,305 @@
+import concourse.mybir as mybir
+from concourse.masks import make_identity
+
+F32 = mybir.dt.float32
+BF16 = mybir.dt.bfloat16
+U32 = mybir.dt.uint32
+U8 = mybir.dt.uint8
+FP8X4 = mybir.dt.float8_e4m3fn_x4
+FUNC = mybir.ActivationFunctionType
+ALU = mybir.AluOpType
+
+P = 128
+AGENTS = 8
+BATCH = 128
+M1 = 512
+F = 1024
+H = 256
+G = 4 * H
+BANK = 512
+PASS_WORDS = 256
+
+FLOPS = 2 * BATCH * AGENTS * (M1 * F + F * G + H * G)
+
+
+def tile_ppo_actor_pa_kernel(tc, f_hid, h0, c0, W2, b2, W_ih, W_hh, b_ih, b_hh, out_0, out_1):
+    nc = tc.nc
+    with (
+        tc.tile_pool(name="keep", bufs=1) as keep,
+        tc.tile_pool(name="raw_hh", bufs=3) as raw_hh,
+        tc.tile_pool(name="raw_ih", bufs=6) as raw_ih,
+        tc.tile_pool(name="stage", bufs=3) as stage,
+        tc.tile_pool(name="units", bufs=8) as units,
+        tc.tile_pool(name="work", bufs=2) as work,
+        tc.psum_pool(name="flip", bufs=4) as flip,
+        tc.psum_pool(name="acc", bufs=4) as acc,
+        tc.manual_schedule(),
+    ):
+        identity = keep.tile([P, P], F32)
+        make_identity(nc, identity[:])
+
+        warm = keep.tile([P, 2], F32)
+        nc.vector.memset(warm[:], 0.0)
+        nc.scalar.activation(out=warm[:, 1:2], in_=warm[:, 0:1], func=FUNC.Sigmoid)
+
+        whh_raw = {}
+        wih_raw = {}
+
+        def load_input_weights(n):
+            for half in range(2):
+                rows = W_ih[n, half * BANK : (half + 1) * BANK, :]
+                wih_raw[(n, half)] = raw_ih.tile([P, 2, 2 * F], BF16, name="wih_raw")
+                nc.sync.dma_start(out=wih_raw[(n, half)][:], in_=rows.rearrange("(q p j) k -> p q (j k)", p=P, j=2))
+
+        def load_recurrent_weights(n):
+            whh_raw[n] = raw_hh.tile([P, 4, 2 * H], BF16, name="whh_raw")
+            nc.sync.dma_start(out=whh_raw[n][:], in_=W_hh[n].rearrange("(q p j) k -> p q (j k)", p=P, j=2))
+
+        vec_rows = keep.tile([P, 2 * P], BF16)
+        nc.vector.memset(vec_rows[:].bitcast(F32), 0.0)
+        b2_rows = keep.tile([P, 4 * P], BF16)
+        nc.vector.memset(b2_rows[:].bitcast(F32), 0.0)
+        nc.sync.dma_start(out=vec_rows[0:32, :], in_=b_ih.rearrange("n (q w) -> (n q) w", w=2 * P))
+        nc.sync.dma_start(out=vec_rows[32:64, :], in_=b_hh.rearrange("n (q w) -> (n q) w", w=2 * P))
+        nc.sync.dma_start(out=b2_rows[0:2, :], in_=b2.rearrange("(c w) -> c w", w=4 * P))
+        fh_raw = keep.tile([P, AGENTS, M1], BF16)
+        nc.sync.dma_start(out=fh_raw[:], in_=f_hid)
+        w2_raw = keep.tile([P, 2, 4 * M1], BF16)
+        nc.sync.dma_start(out=w2_raw[:], in_=W2.rearrange("(c p t) k -> p c (t k)", p=P, t=4))
+        load_input_weights(0)
+        h0_raw = keep.tile([P, AGENTS, H], BF16)
+        nc.sync.dma_start(out=h0_raw[:], in_=h0.rearrange("n b k -> b n k"))
+        load_recurrent_weights(0)
+        load_recurrent_weights(1)
+        load_input_weights(1)
+        c0_sb = keep.tile([P, AGENTS, H], BF16)
+        nc.sync.dma_start(out=c0_sb[:], in_=c0.rearrange("n b k -> b n k"))
+        load_recurrent_weights(2)
+        load_input_weights(2)
+
+        def flip_unit(words, first_word, copy_out):
+            grouped = stage.tile([P, 4 * BANK], BF16, tag="grouped", align_bytes=64)
+            grouped_words = grouped[:].bitcast(F32)
+            for pair in range(2):
+                bank = flip.tile([P, BANK], F32, tag="flip")
+                for a in range(2):
+                    for u in range(2):
+                        nc.tensor.transpose(
+                            bank[:, (2 * a + u) * P : (2 * a + u + 1) * P],
+                            words[:, 2 * pair + a, first_word + u : first_word + PASS_WORDS : 2],
+                            identity[:],
+                        )
+                copy_out(
+                    out=grouped_words[:, pair * BANK : (pair + 1) * BANK].rearrange("p (a c u) -> p a c u", a=2, u=2),
+                    in_=bank[:].rearrange("p (a u c) -> p a c u", a=2, u=2),
+                )
+            return grouped
+
+        def flip_pairs(words, pairs, copy_outs):
+            for half in range(2):
+                bank = flip.tile([P, BANK], F32, tag="flip")
+                for i in range(4):
+                    s = 4 * half + i
+                    nc.tensor.transpose(bank[:, i * P : (i + 1) * P], words[:, s * P : (s + 1) * P], identity[:])
+                copy_outs[half](
+                    out=pairs[:, half * BANK : (half + 1) * BANK, :].rearrange("p c e -> p (c e)"),
+                    in_=bank[:].bitcast(BF16),
+                )
+
+        vec_bank = flip.tile([P, BANK], F32, tag="flip")
+        nc.tensor.transpose(vec_bank[:, 0:P], vec_rows[:].bitcast(F32), identity[:])
+        for u in range(2):
+            nc.tensor.transpose(
+                vec_bank[:, (1 + u) * P : (2 + u) * P], b2_rows[:].bitcast(F32)[:, u : 2 * P : 2], identity[:]
+            )
+        vec_cols = keep.tile([P, 128], F32)
+        nc.vector.tensor_copy(out=vec_cols[:], in_=vec_bank[:].bitcast(BF16)[:, 0:128])
+        gate_bias = keep.tile([P, 64], F32)
+        nc.vector.tensor_tensor(out=gate_bias[:], in0=vec_cols[:, 0:64], in1=vec_cols[:, 64:128], op=ALU.add)
+        b2_cols = keep.tile([P, 8], F32)
+        for u in range(2):
+            nc.vector.tensor_copy(
+                out=b2_cols[:].rearrange("p (c u e) -> p c u e", u=2, e=2)[:, :, u, :],
+                in_=vec_bank[:].bitcast(BF16)[:, 2 * (1 + u) * P : 2 * (1 + u) * P + 4].rearrange("p (c e) -> p c e", e=2),
+            )
+
+        fh_codes = keep.tile([P, AGENTS * BATCH], U32, align_bytes=64)
+        fh_scales = keep.tile([P, AGENTS * BATCH], U8, align_bytes=64)
+        w2_codes = keep.tile([P, F], U32, align_bytes=64)
+        w2_scales = keep.tile([P, F], U8, align_bytes=64)
+        fh_words = fh_raw[:].rearrange("p n k -> p (n k)").bitcast(F32).rearrange("p (s w) -> p s w", s=8)
+        w2_words = w2_raw[:].rearrange("p r k -> p (r k)").bitcast(F32).rearrange("p (s w) -> p s w", s=8)
+        fh_grouped = [flip_unit(fh_words[:, 4 * i : 4 * i + 4, :], 0, nc.scalar.copy) for i in range(2)]
+        for i in range(2):
+            cols = slice(i * BANK, (i + 1) * BANK)
+            nc.vector.quantize_mx(out=fh_codes[:, cols].bitcast(FP8X4), scales=fh_scales[:, cols], in_=fh_grouped[i][:])
+        w2_grouped = [flip_unit(w2_words[:, 4 * i : 4 * i + 4, :], 0, nc.vector.tensor_copy) for i in range(2)]
+        for i in range(2):
+            cols = slice(i * BANK, (i + 1) * BANK)
+            nc.vector.quantize_mx(out=w2_codes[:, cols].bitcast(FP8X4), scales=w2_scales[:, cols], in_=w2_grouped[i][:])
+
+        wih_grouped = {}
+        wih_codes = {}
+        wih_scales = {}
+        whhT = {}
+        hh_sb = {}
+        gates = {}
+        squashed = {}
+        h_c = {}
+
+        def flip_input_weights(n, r):
+            if n == AGENTS:
+                return
+            half, c = divmod(r, 2)
+            words = wih_raw[(n, half)][:].rearrange("p q k -> p (q k)").bitcast(F32).rearrange("p (s w) -> p s w", s=4)
+            wih_grouped[(n, r)] = flip_unit(words, c * PASS_WORDS, nc.scalar.copy)
+
+        def quantise_input_weights(n, r):
+            if n == AGENTS:
+                return
+            wih_codes[(n, r)] = units.tile([P, BANK], U32, name="wih_codes", align_bytes=64)
+            wih_scales[(n, r)] = units.tile([P, BANK], U8, name="wih_scales", align_bytes=64)
+            nc.vector.quantize_mx(
+                out=wih_codes[(n, r)][:].bitcast(FP8X4), scales=wih_scales[(n, r)][:], in_=wih_grouped[(n, r)][:]
+            )
+
+        def flip_recurrent_weights(n):
+            if n == AGENTS:
+                return
+            whhT[n] = work.tile([P, G, 2], BF16, name="whhT")
+            flip_pairs(
+                whh_raw[n][:].rearrange("p q k -> p (q k)").bitcast(F32), whhT[n], [nc.scalar.copy, nc.vector.tensor_copy]
+            )
+
+        def recurrent_group(n, half):
+            hh_bank = acc.tile([P, BANK], F32, tag="acc")
+            for i in range(4):
+                m = 8 * n + 4 * half + i
+                nc.tensor.matmul(
+                    out=hh_bank[:, i * P : (i + 1) * P],
+                    lhsT=gate_bias[:, m : m + 1].to_broadcast([P, P]),
+                    rhs=identity[:],
+                    is_transpose=True,
+                    start=(i == 0),
+                    stop=False,
+                )
+            for e in range(2):
+                nc.tensor.matmul(
+                    out=hh_bank[:],
+                    lhsT=h0T[:, n * BATCH : (n + 1) * BATCH, e],
+                    rhs=whhT[n][:, half * BANK : (half + 1) * BANK, e],
+                    start=False,
+                    stop=(e == 1),
+                )
+            hh_sb[(n, half)] = work.tile([P, BANK], F32, name="hh_sb")
+            nc.vector.tensor_copy(
+                out=hh_sb[(n, half)][:].rearrange("b (q p j) -> b q p j", q=2, j=2),
+                in_=hh_bank[:].rearrange("b (q j p) -> b q p j", q=2, j=2),
+            )
+
+        def input_group(n, half):
+            mx_bank = acc.tile([P, BANK], F32, tag="acc")
+            for c in range(2):
+                nc.tensor.matmul_mx(
+                    out=mx_bank[:],
+                    lhsT=feat_codes[:, c, n * BATCH : (n + 1) * BATCH].bitcast(FP8X4),
+                    lhsT_scale=feat_scales[:, c, n * BATCH : (n + 1) * BATCH],
+                    rhs=wih_codes[(n, 2 * half + c)][:].bitcast(FP8X4),
+                    rhs_scale=wih_scales[(n, 2 * half + c)][:],
+                    start=(c == 0),
+                    stop=(c == 1),
+                )
+            if half == 0:
+                gates[n] = work.tile([P, G], F32, name="gates")
+            nc.vector.tensor_tensor(
+                out=gates[n][:, half * BANK : (half + 1) * BANK].rearrange("b (q p j) -> b q p j", q=2, j=2),
+                in0=mx_bank[:].rearrange("b (q j p) -> b q p j", q=2, j=2),
+                in1=hh_sb[(n, half)][:].rearrange("b (q p j) -> b q p j", q=2, j=2),
+                op=ALU.add,
+            )
+
+        def squash_input_and_forget(n):
+            squashed[n] = work.tile([P, G], F32, name="squashed")
+            nc.scalar.activation(out=squashed[n][:, 0 : 2 * H], in_=gates[n][:, 0 : 2 * H], func=FUNC.Sigmoid)
+
+        def new_state(n):
+            nc.scalar.activation(out=squashed[n][:, 2 * H : 3 * H], in_=gates[n][:, 2 * H : 3 * H], func=FUNC.Tanh)
+            nc.scalar.activation(out=squashed[n][:, 3 * H : 4 * H], in_=gates[n][:, 3 * H : 4 * H], func=FUNC.Sigmoid)
+            h_c[n] = work.tile([P, 2, H], F32, name="h_c")
+            nc.vector.tensor_tensor(out=h_c[n][:, 0, :], in0=squashed[n][:, H : 2 * H], in1=c0_sb[:, n, :], op=ALU.mult)
+            fresh = work.tile([P, H], F32, tag="fresh")
+            nc.vector.tensor_tensor(out=fresh[:], in0=squashed[n][:, 0:H], in1=squashed[n][:, 2 * H : 3 * H], op=ALU.mult)
+            nc.vector.tensor_tensor(out=h_c[n][:, 1, :], in0=h_c[n][:, 0, :], in1=fresh[:], op=ALU.add)
+            nc.sync.dma_start(out=out_1[n], in_=h_c[n][:, 1, :])
+
+        def new_output(n):
+            if n < 0:
+                return
+            tanh_c = work.tile([P, H], F32, tag="tanh_c")
+            nc.scalar.activation(out=tanh_c[:], in_=h_c[n][:, 1, :], func=FUNC.Tanh)
+            nc.vector.tensor_tensor(out=h_c[n][:, 0, :], in0=squashed[n][:, 3 * H : 4 * H], in1=tanh_c[:], op=ALU.mult)
+            nc.sync.dma_start(out=out_0[n], in_=h_c[n][:, 0, :])
+
+        feat_codes = keep.tile([P, 2, AGENTS * BATCH], U32, align_bytes=64)
+        feat_scales = keep.tile([P, 2, AGENTS * BATCH], U8, align_bytes=64)
+        for r in range(4):
+            four_agents, c = divmod(r, 2)
+            cols = slice(four_agents * BANK, (four_agents + 1) * BANK)
+            planes = stage.tile([P, 4, BANK], BF16, tag="planes")
+            for t in range(4):
+                s = 4 * c + t
+                f_bank = acc.tile([P, BANK], F32, tag="acc")
+                nc.tensor.matmul_mx(
+                    out=f_bank[:],
+                    lhsT=w2_codes[:, s * P : (s + 1) * P].bitcast(FP8X4),
+                    lhsT_scale=w2_scales[:, s * P : (s + 1) * P],
+                    rhs=fh_codes[:, cols].bitcast(FP8X4),
+                    rhs_scale=fh_scales[:, cols],
+                    start=True,
+                    stop=True,
+                )
+                if t < 3:
+                    nc.scalar.activation(out=planes[:, t, :], in_=f_bank[:], func=FUNC.Relu, bias=b2_cols[:, s : s + 1])
+                else:
+                    nc.vector.tensor_scalar(
+                        out=planes[:, t, :], in0=f_bank[:], scalar1=b2_cols[:, s : s + 1], scalar2=0.0,
+                        op0=ALU.add, op1=ALU.max,
+                    )
+            flip_input_weights(0, r)
+            feat_grouped = stage.tile([P, BANK, 4], BF16, tag="feat_grouped", align_bytes=64)
+            nc.vector.tensor_copy(
+                out=feat_grouped[:].rearrange("p (c i) t -> p c t i", i=4),
+                in_=planes[:].rearrange("p t (c i) -> p c t i", i=4),
+            )
+            nc.vector.quantize_mx(
+                out=feat_codes[:, c, cols].bitcast(FP8X4),
+                scales=feat_scales[:, c, cols],
+                in_=feat_grouped[:].rearrange("p c t -> p (c t)"),
+            )
+            quantise_input_weights(0, r)
+
+        h0T = keep.tile([P, AGENTS * BATCH, 2], BF16)
+        flip_pairs(h0_raw[:].rearrange("p n k -> p (n k)").bitcast(F32), h0T, [nc.scalar.copy, nc.vector.tensor_copy])
+        flip_recurrent_weights(0)
+
+        for n in range(AGENTS):
+            if n + 3 < AGENTS:
+                load_recurrent_weights(n + 3)
+                load_input_weights(n + 3)
+            flip_input_weights(n + 1, 0)
+            recurrent_group(n, 0)
+            new_output(n - 1)
+            quantise_input_weights(n + 1, 0)
+            flip_input_weights(n + 1, 1)
+            input_group(n, 0)
+            quantise_input_weights(n + 1, 1)
+            flip_input_weights(n + 1, 2)
+            squash_input_and_forget(n)
+            recurrent_group(n, 1)
+            quantise_input_weights(n + 1, 2)
+            flip_input_weights(n + 1, 3)
+            input_group(n, 1)
+            quantise_input_weights(n + 1, 3)
+            flip_recurrent_weights(n + 1)
+            new_state(n)
+        new_output(AGENTS - 1)

@@ -26,13 +26,12 @@ def tile_ppo_actor_pa_kernel(tc, f_hid, h0, c0, W2, b2, W_ih, W_hh, b_ih, b_hh, 
     nc = tc.nc
     with (
         tc.tile_pool(name="keep", bufs=1) as keep,
-        tc.tile_pool(name="raw_hh", bufs=3) as raw_hh,
-        tc.tile_pool(name="raw_ih", bufs=6) as raw_ih,
+        tc.tile_pool(name="raw_hh", bufs=4) as raw_hh,
+        tc.tile_pool(name="raw_ih", bufs=8) as raw_ih,
         tc.tile_pool(name="stage", bufs=3) as stage,
-        tc.tile_pool(name="units", bufs=8) as units,
-        tc.tile_pool(name="work", bufs=2) as work,
-        tc.psum_pool(name="flip", bufs=4) as flip,
-        tc.psum_pool(name="acc", bufs=4) as acc,
+        tc.tile_pool(name="units", bufs=6) as units,
+        tc.tile_pool(name="work", bufs=3) as work,
+        tc.psum_pool(name="banks", bufs=8) as banks,
         tc.manual_schedule(),
     ):
         identity = keep.tile([P, P], F32)
@@ -45,43 +44,57 @@ def tile_ppo_actor_pa_kernel(tc, f_hid, h0, c0, W2, b2, W_ih, W_hh, b_ih, b_hh, 
         whh_raw = {}
         wih_raw = {}
 
-        def load_input_weights(n):
-            for half in range(2):
-                rows = W_ih[n, half * BANK : (half + 1) * BANK, :]
-                wih_raw[(n, half)] = raw_ih.tile([P, 2, 2 * F], BF16, name="wih_raw")
-                nc.sync.dma_start(out=wih_raw[(n, half)][:], in_=rows.rearrange("(q p j) k -> p q (j k)", p=P, j=2))
+        def load_input_weights(n, half):
+            rows = W_ih[n, half * BANK : (half + 1) * BANK, :]
+            wih_raw[(n, half)] = raw_ih.tile([P, 2, 2 * F], BF16, name="wih_raw")
+            nc.sync.dma_start(out=wih_raw[(n, half)][:], in_=rows.rearrange("(q p j) k -> p q (j k)", p=P, j=2))
 
         def load_recurrent_weights(n):
             whh_raw[n] = raw_hh.tile([P, 4, 2 * H], BF16, name="whh_raw")
             nc.sync.dma_start(out=whh_raw[n][:], in_=W_hh[n].rearrange("(q p j) k -> p q (j k)", p=P, j=2))
 
+        fh_raw = [keep.tile([P, 4, M1], BF16, name="fh_raw%d" % i) for i in range(2)]
+        w2_raw = [keep.tile([P, 4, M1], BF16, name="w2_raw%d" % c) for c in range(2)]
         vec_rows = keep.tile([P, 2 * P], BF16)
         nc.vector.memset(vec_rows[:].bitcast(F32), 0.0)
         b2_rows = keep.tile([P, 4 * P], BF16)
         nc.vector.memset(b2_rows[:].bitcast(F32), 0.0)
+        h0_raw = keep.tile([P, AGENTS, H], BF16)
+        c0_sb = keep.tile([P, AGENTS, H], BF16)
+
+        def load_f_hid(i):
+            nc.sync.dma_start(out=fh_raw[i][:], in_=f_hid[:, 4 * i : 4 * i + 4, :])
+
+        def load_feature_weights(c):
+            nc.sync.dma_start(out=w2_raw[c][:], in_=W2[c * BANK : (c + 1) * BANK, :].rearrange("(p t) k -> p t k", t=4))
+
+        load_f_hid(0)
+        load_feature_weights(0)
+        nc.sync.dma_start(out=b2_rows[0:2, :], in_=b2.rearrange("(c w) -> c w", w=4 * P))
         nc.sync.dma_start(out=vec_rows[0:32, :], in_=b_ih.rearrange("n (q w) -> (n q) w", w=2 * P))
         nc.sync.dma_start(out=vec_rows[32:64, :], in_=b_hh.rearrange("n (q w) -> (n q) w", w=2 * P))
-        nc.sync.dma_start(out=b2_rows[0:2, :], in_=b2.rearrange("(c w) -> c w", w=4 * P))
-        fh_raw = keep.tile([P, AGENTS, M1], BF16)
-        nc.sync.dma_start(out=fh_raw[:], in_=f_hid)
-        w2_raw = keep.tile([P, 2, 4 * M1], BF16)
-        nc.sync.dma_start(out=w2_raw[:], in_=W2.rearrange("(c p t) k -> p c (t k)", p=P, t=4))
-        load_input_weights(0)
-        h0_raw = keep.tile([P, AGENTS, H], BF16)
+        load_feature_weights(1)
+        load_input_weights(0, 0)
         nc.sync.dma_start(out=h0_raw[:], in_=h0.rearrange("n b k -> b n k"))
         load_recurrent_weights(0)
-        load_recurrent_weights(1)
-        load_input_weights(1)
-        c0_sb = keep.tile([P, AGENTS, H], BF16)
+        load_input_weights(0, 1)
         nc.sync.dma_start(out=c0_sb[:], in_=c0.rearrange("n b k -> b n k"))
+        load_input_weights(1, 0)
+        load_recurrent_weights(1)
+        load_f_hid(1)
+        load_input_weights(1, 1)
+        load_input_weights(2, 0)
         load_recurrent_weights(2)
-        load_input_weights(2)
+        load_input_weights(2, 1)
+        load_input_weights(3, 0)
+        load_recurrent_weights(3)
+        load_input_weights(3, 1)
 
-        def flip_unit(words, first_word, copy_out):
+        def flip_unit(words, first_word, copy_outs):
             grouped = stage.tile([P, 4 * BANK], BF16, tag="grouped", align_bytes=64)
             grouped_words = grouped[:].bitcast(F32)
             for pair in range(2):
-                bank = flip.tile([P, BANK], F32, tag="flip")
+                bank = banks.tile([P, BANK], F32, tag="bank")
                 for a in range(2):
                     for u in range(2):
                         nc.tensor.transpose(
@@ -89,54 +102,97 @@ def tile_ppo_actor_pa_kernel(tc, f_hid, h0, c0, W2, b2, W_ih, W_hh, b_ih, b_hh, 
                             words[:, 2 * pair + a, first_word + u : first_word + PASS_WORDS : 2],
                             identity[:],
                         )
-                copy_out(
+                copy_outs[pair](
                     out=grouped_words[:, pair * BANK : (pair + 1) * BANK].rearrange("p (a c u) -> p a c u", a=2, u=2),
                     in_=bank[:].rearrange("p (a u c) -> p a c u", a=2, u=2),
                 )
             return grouped
 
-        def flip_pairs(words, pairs, copy_outs):
-            for half in range(2):
-                bank = flip.tile([P, BANK], F32, tag="flip")
-                for i in range(4):
-                    s = 4 * half + i
-                    nc.tensor.transpose(bank[:, i * P : (i + 1) * P], words[:, s * P : (s + 1) * P], identity[:])
-                copy_outs[half](
-                    out=pairs[:, half * BANK : (half + 1) * BANK, :].rearrange("p c e -> p (c e)"),
-                    in_=bank[:].bitcast(BF16),
-                )
+        def flip_pairs(words, pairs, copy_out):
+            bank = banks.tile([P, BANK], F32, tag="bank")
+            for i in range(4):
+                nc.tensor.transpose(bank[:, i * P : (i + 1) * P], words[:, i * P : (i + 1) * P], identity[:])
+            copy_out(out=pairs.rearrange("p c e -> p (c e)"), in_=bank[:].bitcast(BF16))
 
-        vec_bank = flip.tile([P, BANK], F32, tag="flip")
+        SCALAR, VECTOR = nc.scalar.copy, nc.vector.tensor_copy
+
+        fh_codes = keep.tile([P, AGENTS * BATCH], U32, align_bytes=64)
+        fh_scales = keep.tile([P, AGENTS * BATCH], U8, align_bytes=64)
+        w2_codes = keep.tile([P, F], U32, align_bytes=64)
+        w2_scales = keep.tile([P, F], U8, align_bytes=64)
+
+        def pair_words(raw):
+            return raw[:].rearrange("p n k -> p (n k)").bitcast(F32).rearrange("p (s w) -> p s w", s=4)
+
+        def quantise(codes, scales, i, grouped):
+            cols = slice(i * BANK, (i + 1) * BANK)
+            nc.vector.quantize_mx(out=codes[:, cols].bitcast(FP8X4), scales=scales[:, cols], in_=grouped[:])
+
+        fh_grouped = flip_unit(pair_words(fh_raw[0]), 0, [SCALAR, VECTOR])
+        w2_grouped = flip_unit(pair_words(w2_raw[0]), 0, [SCALAR, SCALAR])
+        quantise(fh_codes, fh_scales, 0, fh_grouped)
+
+        vec_bank = banks.tile([P, BANK], F32, tag="bank")
         nc.tensor.transpose(vec_bank[:, 0:P], vec_rows[:].bitcast(F32), identity[:])
         for u in range(2):
             nc.tensor.transpose(
                 vec_bank[:, (1 + u) * P : (2 + u) * P], b2_rows[:].bitcast(F32)[:, u : 2 * P : 2], identity[:]
             )
-        vec_cols = keep.tile([P, 128], F32)
-        nc.vector.tensor_copy(out=vec_cols[:], in_=vec_bank[:].bitcast(BF16)[:, 0:128])
-        gate_bias = keep.tile([P, 64], F32)
-        nc.vector.tensor_tensor(out=gate_bias[:], in0=vec_cols[:, 0:64], in1=vec_cols[:, 64:128], op=ALU.add)
         b2_cols = keep.tile([P, 8], F32)
         for u in range(2):
             nc.vector.tensor_copy(
                 out=b2_cols[:].rearrange("p (c u e) -> p c u e", u=2, e=2)[:, :, u, :],
                 in_=vec_bank[:].bitcast(BF16)[:, 2 * (1 + u) * P : 2 * (1 + u) * P + 4].rearrange("p (c e) -> p c e", e=2),
             )
+        vec_cols = keep.tile([P, 128], F32)
+        nc.vector.tensor_copy(out=vec_cols[:], in_=vec_bank[:].bitcast(BF16)[:, 0:128])
+        quantise(w2_codes, w2_scales, 0, w2_grouped)
+        gate_bias = keep.tile([P, 64], F32)
+        nc.vector.tensor_tensor(out=gate_bias[:], in0=vec_cols[:, 0:64], in1=vec_cols[:, 64:128], op=ALU.add)
 
-        fh_codes = keep.tile([P, AGENTS * BATCH], U32, align_bytes=64)
-        fh_scales = keep.tile([P, AGENTS * BATCH], U8, align_bytes=64)
-        w2_codes = keep.tile([P, F], U32, align_bytes=64)
-        w2_scales = keep.tile([P, F], U8, align_bytes=64)
-        fh_words = fh_raw[:].rearrange("p n k -> p (n k)").bitcast(F32).rearrange("p (s w) -> p s w", s=8)
-        w2_words = w2_raw[:].rearrange("p r k -> p (r k)").bitcast(F32).rearrange("p (s w) -> p s w", s=8)
-        fh_grouped = [flip_unit(fh_words[:, 4 * i : 4 * i + 4, :], 0, nc.scalar.copy) for i in range(2)]
-        for i in range(2):
-            cols = slice(i * BANK, (i + 1) * BANK)
-            nc.vector.quantize_mx(out=fh_codes[:, cols].bitcast(FP8X4), scales=fh_scales[:, cols], in_=fh_grouped[i][:])
-        w2_grouped = [flip_unit(w2_words[:, 4 * i : 4 * i + 4, :], 0, nc.vector.tensor_copy) for i in range(2)]
-        for i in range(2):
-            cols = slice(i * BANK, (i + 1) * BANK)
-            nc.vector.quantize_mx(out=w2_codes[:, cols].bitcast(FP8X4), scales=w2_scales[:, cols], in_=w2_grouped[i][:])
+        feat_codes = keep.tile([P, 2, AGENTS * BATCH], U32, align_bytes=64)
+        feat_scales = keep.tile([P, 2, AGENTS * BATCH], U8, align_bytes=64)
+        planes = {}
+        feat_grouped = {}
+
+        def feature_planes(four_agents, c, ts):
+            cols = slice(four_agents * BANK, (four_agents + 1) * BANK)
+            if ts[0] == 0:
+                planes[(four_agents, c)] = stage.tile([P, 4, BANK], BF16, name="planes")
+            for t in ts:
+                s = 4 * c + t
+                f_bank = banks.tile([P, BANK], F32, tag="bank")
+                nc.tensor.matmul_mx(
+                    out=f_bank[:],
+                    lhsT=w2_codes[:, s * P : (s + 1) * P].bitcast(FP8X4),
+                    lhsT_scale=w2_scales[:, s * P : (s + 1) * P],
+                    rhs=fh_codes[:, cols].bitcast(FP8X4),
+                    rhs_scale=fh_scales[:, cols],
+                    start=True,
+                    stop=True,
+                )
+                out = planes[(four_agents, c)][:, t, :]
+                if t < 3:
+                    nc.scalar.activation(out=out, in_=f_bank[:], func=FUNC.Relu, bias=b2_cols[:, s : s + 1])
+                else:
+                    nc.vector.tensor_scalar(
+                        out=out, in0=f_bank[:], scalar1=b2_cols[:, s : s + 1], scalar2=0.0, op0=ALU.add, op1=ALU.max
+                    )
+
+        def interleave_features(four_agents, c):
+            feat_grouped[(four_agents, c)] = stage.tile([P, BANK, 4], BF16, name="feat_grouped", align_bytes=64)
+            nc.vector.tensor_copy(
+                out=feat_grouped[(four_agents, c)][:].rearrange("p (c i) t -> p c t i", i=4),
+                in_=planes[(four_agents, c)][:].rearrange("p t (c i) -> p c t i", i=4),
+            )
+
+        def quantise_features(four_agents, c):
+            cols = slice(four_agents * BANK, (four_agents + 1) * BANK)
+            nc.vector.quantize_mx(
+                out=feat_codes[:, c, cols].bitcast(FP8X4),
+                scales=feat_scales[:, c, cols],
+                in_=feat_grouped[(four_agents, c)][:].rearrange("p c t -> p (c t)"),
+            )
 
         wih_grouped = {}
         wih_codes = {}
@@ -147,32 +203,28 @@ def tile_ppo_actor_pa_kernel(tc, f_hid, h0, c0, W2, b2, W_ih, W_hh, b_ih, b_hh, 
         squashed = {}
         h_c = {}
 
-        def flip_input_weights(n, r):
-            if n == AGENTS:
-                return
-            half, c = divmod(r, 2)
-            words = wih_raw[(n, half)][:].rearrange("p q k -> p (q k)").bitcast(F32).rearrange("p (s w) -> p s w", s=4)
-            wih_grouped[(n, r)] = flip_unit(words, c * PASS_WORDS, nc.scalar.copy)
+        def flip_input_weights(n, half, c):
+            if n < AGENTS:
+                wih_grouped[(n, half, c)] = flip_unit(pair_words(wih_raw[(n, half)]), c * PASS_WORDS, [SCALAR, SCALAR])
 
-        def quantise_input_weights(n, r):
+        def quantise_input_weights(n, half, c):
             if n == AGENTS:
                 return
-            wih_codes[(n, r)] = units.tile([P, BANK], U32, name="wih_codes", align_bytes=64)
-            wih_scales[(n, r)] = units.tile([P, BANK], U8, name="wih_scales", align_bytes=64)
-            nc.vector.quantize_mx(
-                out=wih_codes[(n, r)][:].bitcast(FP8X4), scales=wih_scales[(n, r)][:], in_=wih_grouped[(n, r)][:]
-            )
+            wih_codes[(n, half, c)] = units.tile([P, BANK], U32, name="wih_codes", align_bytes=64)
+            wih_scales[(n, half, c)] = units.tile([P, BANK], U8, name="wih_scales", align_bytes=64)
+            quantise(wih_codes[(n, half, c)], wih_scales[(n, half, c)], 0, wih_grouped[(n, half, c)])
 
-        def flip_recurrent_weights(n):
+        def flip_recurrent_weights(n, half, copy_out):
             if n == AGENTS:
                 return
-            whhT[n] = work.tile([P, G, 2], BF16, name="whhT")
-            flip_pairs(
-                whh_raw[n][:].rearrange("p q k -> p (q k)").bitcast(F32), whhT[n], [nc.scalar.copy, nc.vector.tensor_copy]
-            )
+            if half == 0:
+                whhT[n] = work.tile([P, G, 2], BF16, name="whhT")
+            words = whh_raw[n][:].rearrange("p q k -> p (q k)").bitcast(F32)
+            cols = slice(half * BANK, (half + 1) * BANK)
+            flip_pairs(words[:, cols], whhT[n][:, cols, :], copy_out)
 
         def recurrent_group(n, half):
-            hh_bank = acc.tile([P, BANK], F32, tag="acc")
+            hh_bank = banks.tile([P, BANK], F32, tag="bank")
             for i in range(4):
                 m = 8 * n + 4 * half + i
                 nc.tensor.matmul(
@@ -198,14 +250,14 @@ def tile_ppo_actor_pa_kernel(tc, f_hid, h0, c0, W2, b2, W_ih, W_hh, b_ih, b_hh, 
             )
 
         def input_group(n, half):
-            mx_bank = acc.tile([P, BANK], F32, tag="acc")
+            mx_bank = banks.tile([P, BANK], F32, tag="bank")
             for c in range(2):
                 nc.tensor.matmul_mx(
                     out=mx_bank[:],
                     lhsT=feat_codes[:, c, n * BATCH : (n + 1) * BATCH].bitcast(FP8X4),
                     lhsT_scale=feat_scales[:, c, n * BATCH : (n + 1) * BATCH],
-                    rhs=wih_codes[(n, 2 * half + c)][:].bitcast(FP8X4),
-                    rhs_scale=wih_scales[(n, 2 * half + c)][:],
+                    rhs=wih_codes[(n, half, c)][:].bitcast(FP8X4),
+                    rhs_scale=wih_scales[(n, half, c)][:],
                     start=(c == 0),
                     stop=(c == 1),
                 )
@@ -221,85 +273,99 @@ def tile_ppo_actor_pa_kernel(tc, f_hid, h0, c0, W2, b2, W_ih, W_hh, b_ih, b_hh, 
         def squash_input_and_forget(n):
             squashed[n] = work.tile([P, G], F32, name="squashed")
             nc.scalar.activation(out=squashed[n][:, 0 : 2 * H], in_=gates[n][:, 0 : 2 * H], func=FUNC.Sigmoid)
+            h_c[n] = work.tile([P, 2, H], F32, name="h_c")
 
-        def new_state(n):
+        def keep_old_state(n):
+            nc.vector.tensor_tensor(out=h_c[n][:, 0, :], in0=squashed[n][:, H : 2 * H], in1=c0_sb[:, n, :], op=ALU.mult)
+
+        def squash_candidate_and_output(n):
             nc.scalar.activation(out=squashed[n][:, 2 * H : 3 * H], in_=gates[n][:, 2 * H : 3 * H], func=FUNC.Tanh)
             nc.scalar.activation(out=squashed[n][:, 3 * H : 4 * H], in_=gates[n][:, 3 * H : 4 * H], func=FUNC.Sigmoid)
-            h_c[n] = work.tile([P, 2, H], F32, name="h_c")
-            nc.vector.tensor_tensor(out=h_c[n][:, 0, :], in0=squashed[n][:, H : 2 * H], in1=c0_sb[:, n, :], op=ALU.mult)
-            fresh = work.tile([P, H], F32, tag="fresh")
+
+        def new_state(n):
+            fresh = work.tile([P, H], F32, name="fresh")
             nc.vector.tensor_tensor(out=fresh[:], in0=squashed[n][:, 0:H], in1=squashed[n][:, 2 * H : 3 * H], op=ALU.mult)
             nc.vector.tensor_tensor(out=h_c[n][:, 1, :], in0=h_c[n][:, 0, :], in1=fresh[:], op=ALU.add)
             nc.sync.dma_start(out=out_1[n], in_=h_c[n][:, 1, :])
 
+        tanh_c = {}
+
+        def squash_state(n):
+            tanh_c[n] = work.tile([P, H], F32, name="tanh_c")
+            nc.scalar.activation(out=tanh_c[n][:], in_=h_c[n][:, 1, :], func=FUNC.Tanh)
+
         def new_output(n):
-            if n < 0:
-                return
-            tanh_c = work.tile([P, H], F32, tag="tanh_c")
-            nc.scalar.activation(out=tanh_c[:], in_=h_c[n][:, 1, :], func=FUNC.Tanh)
-            nc.vector.tensor_tensor(out=h_c[n][:, 0, :], in0=squashed[n][:, 3 * H : 4 * H], in1=tanh_c[:], op=ALU.mult)
+            nc.vector.tensor_tensor(out=h_c[n][:, 0, :], in0=squashed[n][:, 3 * H : 4 * H], in1=tanh_c[n][:], op=ALU.mult)
             nc.sync.dma_start(out=out_0[n], in_=h_c[n][:, 0, :])
 
-        feat_codes = keep.tile([P, 2, AGENTS * BATCH], U32, align_bytes=64)
-        feat_scales = keep.tile([P, 2, AGENTS * BATCH], U8, align_bytes=64)
-        for r in range(4):
-            four_agents, c = divmod(r, 2)
-            cols = slice(four_agents * BANK, (four_agents + 1) * BANK)
-            planes = stage.tile([P, 4, BANK], BF16, tag="planes")
-            for t in range(4):
-                s = 4 * c + t
-                f_bank = acc.tile([P, BANK], F32, tag="acc")
-                nc.tensor.matmul_mx(
-                    out=f_bank[:],
-                    lhsT=w2_codes[:, s * P : (s + 1) * P].bitcast(FP8X4),
-                    lhsT_scale=w2_scales[:, s * P : (s + 1) * P],
-                    rhs=fh_codes[:, cols].bitcast(FP8X4),
-                    rhs_scale=fh_scales[:, cols],
-                    start=True,
-                    stop=True,
-                )
-                if t < 3:
-                    nc.scalar.activation(out=planes[:, t, :], in_=f_bank[:], func=FUNC.Relu, bias=b2_cols[:, s : s + 1])
-                else:
-                    nc.vector.tensor_scalar(
-                        out=planes[:, t, :], in0=f_bank[:], scalar1=b2_cols[:, s : s + 1], scalar2=0.0,
-                        op0=ALU.add, op1=ALU.max,
-                    )
-            flip_input_weights(0, r)
-            feat_grouped = stage.tile([P, BANK, 4], BF16, tag="feat_grouped", align_bytes=64)
-            nc.vector.tensor_copy(
-                out=feat_grouped[:].rearrange("p (c i) t -> p c t i", i=4),
-                in_=planes[:].rearrange("p t (c i) -> p c t i", i=4),
-            )
-            nc.vector.quantize_mx(
-                out=feat_codes[:, c, cols].bitcast(FP8X4),
-                scales=feat_scales[:, c, cols],
-                in_=feat_grouped[:].rearrange("p c t -> p (c t)"),
-            )
-            quantise_input_weights(0, r)
-
+        feature_planes(0, 0, [0, 1, 2, 3])
+        w2_grouped = flip_unit(pair_words(w2_raw[1]), 0, [SCALAR, VECTOR])
+        quantise(w2_codes, w2_scales, 1, w2_grouped)
+        interleave_features(0, 0)
+        feature_planes(0, 1, [0, 1, 2, 3])
+        flip_input_weights(0, 0, 0)
+        quantise_features(0, 0)
+        interleave_features(0, 1)
+        flip_input_weights(0, 0, 1)
+        quantise_input_weights(0, 0, 0)
+        quantise_features(0, 1)
         h0T = keep.tile([P, AGENTS * BATCH, 2], BF16)
-        flip_pairs(h0_raw[:].rearrange("p n k -> p (n k)").bitcast(F32), h0T, [nc.scalar.copy, nc.vector.tensor_copy])
-        flip_recurrent_weights(0)
+        h0_words = h0_raw[:].rearrange("p n k -> p (n k)").bitcast(F32)
+        flip_pairs(h0_words[:, 0:BANK], h0T[:, 0:BANK, :], VECTOR)
+        flip_recurrent_weights(0, 0, VECTOR)
+        flip_recurrent_weights(0, 1, VECTOR)
+        quantise_input_weights(0, 0, 1)
 
-        for n in range(AGENTS):
-            if n + 3 < AGENTS:
-                load_recurrent_weights(n + 3)
-                load_input_weights(n + 3)
-            flip_input_weights(n + 1, 0)
-            recurrent_group(n, 0)
-            new_output(n - 1)
-            quantise_input_weights(n + 1, 0)
-            flip_input_weights(n + 1, 1)
-            input_group(n, 0)
-            quantise_input_weights(n + 1, 1)
-            flip_input_weights(n + 1, 2)
-            squash_input_and_forget(n)
-            recurrent_group(n, 1)
-            quantise_input_weights(n + 1, 2)
-            flip_input_weights(n + 1, 3)
-            input_group(n, 1)
-            quantise_input_weights(n + 1, 3)
-            flip_recurrent_weights(n + 1)
-            new_state(n)
-        new_output(AGENTS - 1)
+        def feature_work(step, late):
+            if not late:
+                if step == 1:
+                    fh_late.append(flip_unit(pair_words(fh_raw[1]), 0, [SCALAR, VECTOR]))
+                    flip_pairs(h0_words[:, BANK : 2 * BANK], h0T[:, BANK : 2 * BANK, :], VECTOR)
+                return
+            if step == 1:
+                quantise(fh_codes, fh_scales, 1, fh_late[0])
+            elif step in (2, 3, 4, 5):
+                c, second = divmod(step - 2, 2)
+                feature_planes(1, c, [2, 3] if second else [0, 1])
+                if second:
+                    interleave_features(1, c)
+                    quantise_features(1, c)
+
+        fh_late = []
+        for step in range(2 * AGENTS):
+            n, half = divmod(step, 2)
+            m, mhalf = divmod(step + 1, 2)
+            flip_input_weights(m, mhalf, 0)
+            flip_input_weights(m, mhalf, 1)
+            quantise_input_weights(m, mhalf, 0)
+            if half == 0 and n + 4 < AGENTS:
+                load_input_weights(n + 4, 0)
+                load_recurrent_weights(n + 4)
+                load_input_weights(n + 4, 1)
+            if half == 1:
+                if n > 0:
+                    new_state(n - 1)
+                squash_input_and_forget(n)
+                if n > 0:
+                    squash_state(n - 1)
+            else:
+                if n > 1:
+                    new_output(n - 2)
+                if n > 0:
+                    keep_old_state(n - 1)
+                    squash_candidate_and_output(n - 1)
+            feature_work(step, False)
+            if half == 1:
+                flip_recurrent_weights(n + 1, 0, VECTOR)
+                flip_recurrent_weights(n + 1, 1, SCALAR)
+            recurrent_group(n, half)
+            quantise_input_weights(m, mhalf, 1)
+            input_group(n, half)
+            feature_work(step, True)
+        new_output(AGENTS - 2)
+        keep_old_state(AGENTS - 1)
+        n = AGENTS - 1
+        squash_candidate_and_output(n)
+        new_state(n)
+        squash_state(n)
+        new_output(n)

@@ -19,6 +19,8 @@ G = 4 * H
 BANK = 512
 PASS_WORDS = 256
 
+BIAS_BY_TRANSPOSE = 2
+
 FLOPS = 2 * BATCH * AGENTS * (M1 * F + F * G + H * G)
 
 
@@ -26,8 +28,8 @@ def tile_ppo_actor_pa_kernel(tc, f_hid, h0, c0, W2, b2, W_ih, W_hh, b_ih, b_hh, 
     nc = tc.nc
     with (
         tc.tile_pool(name="keep", bufs=1) as keep,
-        tc.tile_pool(name="raw_hh", bufs=4) as raw_hh,
-        tc.tile_pool(name="raw_ih", bufs=8) as raw_ih,
+        tc.tile_pool(name="raw_hh", bufs=3) as raw_hh,
+        tc.tile_pool(name="raw_ih", bufs=6) as raw_ih,
         tc.tile_pool(name="stage", bufs=3) as stage,
         tc.tile_pool(name="units", bufs=6) as units,
         tc.tile_pool(name="work", bufs=3) as work,
@@ -62,6 +64,11 @@ def tile_ppo_actor_pa_kernel(tc, f_hid, h0, c0, W2, b2, W_ih, W_hh, b_ih, b_hh, 
         h0_raw = keep.tile([P, AGENTS, H], BF16)
         c0_sb = keep.tile([P, AGENTS, H], BF16)
 
+        bias_rows = keep.tile([P, (AGENTS - BIAS_BY_TRANSPOSE) * G], BF16)
+        nc.gpsimd.memset(bias_rows[:].bitcast(F32), 0.0)
+        ones = keep.tile([P, P], BF16)
+        nc.gpsimd.memset(ones[:], 1.0)
+
         def load_f_hid(i):
             nc.sync.dma_start(out=fh_raw[i][:], in_=f_hid[:, 4 * i : 4 * i + 4, :])
 
@@ -80,15 +87,16 @@ def tile_ppo_actor_pa_kernel(tc, f_hid, h0, c0, W2, b2, W_ih, W_hh, b_ih, b_hh, 
         load_input_weights(0, 1)
         nc.sync.dma_start(out=c0_sb[:], in_=c0.rearrange("n b k -> b n k"))
         load_input_weights(1, 0)
+        for row, bias in ((0, b_ih), (1, b_hh)):
+            nc.sync.dma_start(
+                out=bias_rows[row : row + 1, :], in_=bias[BIAS_BY_TRANSPOSE:AGENTS, :].rearrange("(o n) g -> o (n g)", o=1)
+            )
         load_recurrent_weights(1)
         load_f_hid(1)
         load_input_weights(1, 1)
         load_input_weights(2, 0)
         load_recurrent_weights(2)
         load_input_weights(2, 1)
-        load_input_weights(3, 0)
-        load_recurrent_weights(3)
-        load_input_weights(3, 1)
 
         def flip_unit(words, first_word, copy_outs):
             grouped = stage.tile([P, 4 * BANK], BF16, tag="grouped", align_bytes=64)
@@ -225,14 +233,24 @@ def tile_ppo_actor_pa_kernel(tc, f_hid, h0, c0, W2, b2, W_ih, W_hh, b_ih, b_hh, 
 
         def recurrent_group(n, half):
             hh_bank = banks.tile([P, BANK], F32, tag="bank")
-            for i in range(4):
-                m = 8 * n + 4 * half + i
+            if n < BIAS_BY_TRANSPOSE:
+                for i in range(4):
+                    m = 8 * n + 4 * half + i
+                    nc.tensor.matmul(
+                        out=hh_bank[:, i * P : (i + 1) * P],
+                        lhsT=gate_bias[:, m : m + 1].to_broadcast([P, P]),
+                        rhs=identity[:],
+                        is_transpose=True,
+                        start=(i == 0),
+                        stop=False,
+                    )
+            else:
+                first = (n - BIAS_BY_TRANSPOSE) * G + half * BANK
                 nc.tensor.matmul(
-                    out=hh_bank[:, i * P : (i + 1) * P],
-                    lhsT=gate_bias[:, m : m + 1].to_broadcast([P, P]),
-                    rhs=identity[:],
-                    is_transpose=True,
-                    start=(i == 0),
+                    out=hh_bank[:],
+                    lhsT=ones[:],
+                    rhs=bias_rows[:, first : first + BANK].rearrange("k (q p j) -> k q j p", q=2, j=2),
+                    start=True,
                     stop=False,
                 )
             for e in range(2):
@@ -336,31 +354,30 @@ def tile_ppo_actor_pa_kernel(tc, f_hid, h0, c0, W2, b2, W_ih, W_hh, b_ih, b_hh, 
             n, half = divmod(step, 2)
             m, mhalf = divmod(step + 1, 2)
             flip_input_weights(m, mhalf, 0)
-            flip_input_weights(m, mhalf, 1)
-            quantise_input_weights(m, mhalf, 0)
-            if half == 0 and n + 4 < AGENTS:
-                load_input_weights(n + 4, 0)
-                load_recurrent_weights(n + 4)
-                load_input_weights(n + 4, 1)
+            if half == 0 and n + 3 < AGENTS:
+                load_input_weights(n + 3, 0)
+                load_recurrent_weights(n + 3)
             if half == 1:
                 if n > 0:
                     new_state(n - 1)
                 squash_input_and_forget(n)
-                if n > 0:
-                    squash_state(n - 1)
             else:
                 if n > 1:
                     new_output(n - 2)
                 if n > 0:
                     keep_old_state(n - 1)
                     squash_candidate_and_output(n - 1)
-            feature_work(step, False)
-            if half == 1:
-                flip_recurrent_weights(n + 1, 0, VECTOR)
-                flip_recurrent_weights(n + 1, 1, SCALAR)
             recurrent_group(n, half)
-            quantise_input_weights(m, mhalf, 1)
+            quantise_input_weights(m, mhalf, 0)
+            flip_input_weights(m, mhalf, 1)
+            if half == 0 and n + 3 < AGENTS:
+                load_input_weights(n + 3, 1)
+            flip_recurrent_weights(n + 1, half, VECTOR if half else SCALAR)
+            feature_work(step, False)
+            if half == 1 and n > 0:
+                squash_state(n - 1)
             input_group(n, half)
+            quantise_input_weights(m, mhalf, 1)
             feature_work(step, True)
         new_output(AGENTS - 2)
         keep_old_state(AGENTS - 1)

@@ -21,6 +21,8 @@ PASS_WORDS = 256
 
 BIAS_BY_TRANSPOSE = 2
 
+AGENT_GROUPS = ((0, 2), (2, 2), (4, 4))
+
 FLOPS = 2 * BATCH * AGENTS * (M1 * F + F * G + H * G)
 
 
@@ -30,8 +32,8 @@ def tile_ppo_actor_pa_kernel(tc, f_hid, h0, c0, W2, b2, W_ih, W_hh, b_ih, b_hh, 
         tc.tile_pool(name="keep", bufs=1) as keep,
         tc.tile_pool(name="raw_hh", bufs=3) as raw_hh,
         tc.tile_pool(name="raw_ih", bufs=6) as raw_ih,
-        tc.tile_pool(name="stage", bufs=3) as stage,
-        tc.tile_pool(name="units", bufs=6) as units,
+        tc.tile_pool(name="stage", bufs=2) as stage,
+        tc.tile_pool(name="units", bufs=3) as units,
         tc.tile_pool(name="work", bufs=3) as work,
         tc.psum_pool(name="banks", bufs=8) as banks,
         tc.manual_schedule(),
@@ -55,7 +57,7 @@ def tile_ppo_actor_pa_kernel(tc, f_hid, h0, c0, W2, b2, W_ih, W_hh, b_ih, b_hh, 
             whh_raw[n] = raw_hh.tile([P, 4, 2 * H], BF16, name="whh_raw")
             nc.sync.dma_start(out=whh_raw[n][:], in_=W_hh[n].rearrange("(q p j) k -> p q (j k)", p=P, j=2))
 
-        fh_raw = [keep.tile([P, 4, M1], BF16, name="fh_raw%d" % i) for i in range(2)]
+        fh_raw = {first: keep.tile([P, count, M1], BF16, name="fh_raw%d" % first) for first, count in AGENT_GROUPS}
         w2_raw = [keep.tile([P, 4, M1], BF16, name="w2_raw%d" % c) for c in range(2)]
         vec_rows = keep.tile([P, 2 * P], BF16)
         nc.vector.memset(vec_rows[:].bitcast(F32), 0.0)
@@ -69,52 +71,55 @@ def tile_ppo_actor_pa_kernel(tc, f_hid, h0, c0, W2, b2, W_ih, W_hh, b_ih, b_hh, 
         ones = keep.tile([P, P], BF16)
         nc.gpsimd.memset(ones[:], 1.0)
 
-        def load_f_hid(i):
-            nc.sync.dma_start(out=fh_raw[i][:], in_=f_hid[:, 4 * i : 4 * i + 4, :])
+        def load_f_hid(first, count):
+            nc.sync.dma_start(out=fh_raw[first][:], in_=f_hid[:, first : first + count, :])
+
+        def load_state(tile, state, first):
+            agents = slice(first, first + 4)
+            nc.sync.dma_start(out=tile[:, agents, :], in_=state[agents].rearrange("n b k -> b n k"))
 
         def load_feature_weights(c):
             nc.sync.dma_start(out=w2_raw[c][:], in_=W2[c * BANK : (c + 1) * BANK, :].rearrange("(p t) k -> p t k", t=4))
 
-        load_f_hid(0)
+        load_f_hid(*AGENT_GROUPS[0])
         load_feature_weights(0)
         nc.sync.dma_start(out=b2_rows[0:2, :], in_=b2.rearrange("(c w) -> c w", w=4 * P))
         nc.sync.dma_start(out=vec_rows[0:32, :], in_=b_ih.rearrange("n (q w) -> (n q) w", w=2 * P))
         nc.sync.dma_start(out=vec_rows[32:64, :], in_=b_hh.rearrange("n (q w) -> (n q) w", w=2 * P))
         load_feature_weights(1)
         load_input_weights(0, 0)
-        nc.sync.dma_start(out=h0_raw[:], in_=h0.rearrange("n b k -> b n k"))
+        load_state(h0_raw, h0, 0)
         load_recurrent_weights(0)
         load_input_weights(0, 1)
-        nc.sync.dma_start(out=c0_sb[:], in_=c0.rearrange("n b k -> b n k"))
+        load_f_hid(*AGENT_GROUPS[1])
+        load_recurrent_weights(1)
         load_input_weights(1, 0)
+        load_state(c0_sb, c0, 0)
         for row, bias in ((0, b_ih), (1, b_hh)):
             nc.sync.dma_start(
                 out=bias_rows[row : row + 1, :], in_=bias[BIAS_BY_TRANSPOSE:AGENTS, :].rearrange("(o n) g -> o (n g)", o=1)
             )
-        load_recurrent_weights(1)
-        load_f_hid(1)
         load_input_weights(1, 1)
-        load_input_weights(2, 0)
         load_recurrent_weights(2)
+        load_f_hid(*AGENT_GROUPS[2])
+        load_state(h0_raw, h0, 4)
+        load_input_weights(2, 0)
         load_input_weights(2, 1)
+        load_state(c0_sb, c0, 4)
 
-        def flip_unit(words, first_word, copy_outs):
-            grouped = stage.tile([P, 4 * BANK], BF16, tag="grouped", align_bytes=64)
-            grouped_words = grouped[:].bitcast(F32)
-            for pair in range(2):
-                bank = banks.tile([P, BANK], F32, tag="bank")
-                for a in range(2):
-                    for u in range(2):
-                        nc.tensor.transpose(
-                            bank[:, (2 * a + u) * P : (2 * a + u + 1) * P],
-                            words[:, 2 * pair + a, first_word + u : first_word + PASS_WORDS : 2],
-                            identity[:],
-                        )
-                copy_outs[pair](
-                    out=grouped_words[:, pair * BANK : (pair + 1) * BANK].rearrange("p (a c u) -> p a c u", a=2, u=2),
-                    in_=bank[:].rearrange("p (a u c) -> p a c u", a=2, u=2),
-                )
-            return grouped
+        def flip_bank(words, word, grouped_words, copy_out):
+            bank = banks.tile([P, BANK], F32, tag="bank")
+            for a in range(2):
+                for u in range(2):
+                    nc.tensor.transpose(
+                        bank[:, (2 * a + u) * P : (2 * a + u + 1) * P],
+                        words[:, a, word + u : word + PASS_WORDS : 2],
+                        identity[:],
+                    )
+            copy_out(
+                out=grouped_words.rearrange("p (a c u) -> p a c u", a=2, u=2),
+                in_=bank[:].rearrange("p (a u c) -> p a c u", a=2, u=2),
+            )
 
         def flip_pairs(words, pairs, copy_out):
             bank = banks.tile([P, BANK], F32, tag="bank")
@@ -122,23 +127,34 @@ def tile_ppo_actor_pa_kernel(tc, f_hid, h0, c0, W2, b2, W_ih, W_hh, b_ih, b_hh, 
                 nc.tensor.transpose(bank[:, i * P : (i + 1) * P], words[:, i * P : (i + 1) * P], identity[:])
             copy_out(out=pairs.rearrange("p c e -> p (c e)"), in_=bank[:].bitcast(BF16))
 
-        SCALAR, VECTOR = nc.scalar.copy, nc.vector.tensor_copy
+        SCALAR, VECTOR, GPSIMD = nc.scalar.copy, nc.vector.tensor_copy, nc.gpsimd.tensor_copy
 
         fh_codes = keep.tile([P, AGENTS * BATCH], U32, align_bytes=64)
         fh_scales = keep.tile([P, AGENTS * BATCH], U8, align_bytes=64)
         w2_codes = keep.tile([P, F], U32, align_bytes=64)
         w2_scales = keep.tile([P, F], U8, align_bytes=64)
 
-        def pair_words(raw):
-            return raw[:].rearrange("p n k -> p (n k)").bitcast(F32).rearrange("p (s w) -> p s w", s=4)
+        def blocks_of_words(raw, count):
+            return raw[:].rearrange("p n k -> p (n k)").bitcast(F32).rearrange("p (s w) -> p s w", s=count)
 
-        def quantise(codes, scales, i, grouped):
-            cols = slice(i * BANK, (i + 1) * BANK)
-            nc.vector.quantize_mx(out=codes[:, cols].bitcast(FP8X4), scales=scales[:, cols], in_=grouped[:])
+        def quantise(codes, scales, first, grouped):
+            cols = slice(first, first + grouped.shape[1] // 4)
+            nc.vector.quantize_mx(out=codes[:, cols].bitcast(FP8X4), scales=scales[:, cols], in_=grouped)
 
-        fh_grouped = flip_unit(pair_words(fh_raw[0]), 0, [SCALAR, VECTOR])
-        w2_grouped = flip_unit(pair_words(w2_raw[0]), 0, [SCALAR, SCALAR])
+        def flip_rows(raw, count, copy_outs):
+            grouped = stage.tile([P, count * 4 * P], BF16, name="grouped_rows", align_bytes=64)
+            grouped_words = grouped[:].bitcast(F32)
+            words = blocks_of_words(raw, count)
+            for i in range(count // 2):
+                cols = slice(i * BANK, (i + 1) * BANK)
+                flip_bank(words[:, 2 * i : 2 * i + 2, :], 0, grouped_words[:, cols], copy_outs[i])
+            return grouped[:]
+
+        fh_grouped = flip_rows(fh_raw[0], 2, [SCALAR])
+        w2_grouped = [flip_rows(w2_raw[0], 4, [SCALAR, SCALAR])]
         quantise(fh_codes, fh_scales, 0, fh_grouped)
+        w2_grouped.append(flip_rows(w2_raw[1], 4, [SCALAR, VECTOR]))
+        quantise(w2_codes, w2_scales, 0, w2_grouped[0])
 
         vec_bank = banks.tile([P, BANK], F32, tag="bank")
         nc.tensor.transpose(vec_bank[:, 0:P], vec_rows[:].bitcast(F32), identity[:])
@@ -154,7 +170,7 @@ def tile_ppo_actor_pa_kernel(tc, f_hid, h0, c0, W2, b2, W_ih, W_hh, b_ih, b_hh, 
             )
         vec_cols = keep.tile([P, 128], F32)
         nc.vector.tensor_copy(out=vec_cols[:], in_=vec_bank[:].bitcast(BF16)[:, 0:128])
-        quantise(w2_codes, w2_scales, 0, w2_grouped)
+        quantise(w2_codes, w2_scales, BANK, w2_grouped[1])
         gate_bias = keep.tile([P, 64], F32)
         nc.vector.tensor_tensor(out=gate_bias[:], in0=vec_cols[:, 0:64], in1=vec_cols[:, 64:128], op=ALU.add)
 
@@ -163,43 +179,51 @@ def tile_ppo_actor_pa_kernel(tc, f_hid, h0, c0, W2, b2, W_ih, W_hh, b_ih, b_hh, 
         planes = {}
         feat_grouped = {}
 
-        def feature_planes(four_agents, c, ts):
-            cols = slice(four_agents * BANK, (four_agents + 1) * BANK)
+        def feature_planes(group, c, ts):
+            first, count = AGENT_GROUPS[group]
+            n = count * BATCH
+            cols = slice(first * BATCH, first * BATCH + n)
             if ts[0] == 0:
-                planes[(four_agents, c)] = stage.tile([P, 4, BANK], BF16, name="planes")
-            for t in ts:
-                s = 4 * c + t
+                planes[(group, c)] = stage.tile([P, 4, n], BF16, name="planes")
+            for i in range(0, len(ts), BANK // n):
                 f_bank = banks.tile([P, BANK], F32, tag="bank")
-                nc.tensor.matmul_mx(
-                    out=f_bank[:],
-                    lhsT=w2_codes[:, s * P : (s + 1) * P].bitcast(FP8X4),
-                    lhsT_scale=w2_scales[:, s * P : (s + 1) * P],
-                    rhs=fh_codes[:, cols].bitcast(FP8X4),
-                    rhs_scale=fh_scales[:, cols],
-                    start=True,
-                    stop=True,
-                )
-                out = planes[(four_agents, c)][:, t, :]
-                if t < 3:
-                    nc.scalar.activation(out=out, in_=f_bank[:], func=FUNC.Relu, bias=b2_cols[:, s : s + 1])
-                else:
-                    nc.vector.tensor_scalar(
-                        out=out, in0=f_bank[:], scalar1=b2_cols[:, s : s + 1], scalar2=0.0, op0=ALU.add, op1=ALU.max
+                parts = [(t, f_bank[:, k * n : (k + 1) * n]) for k, t in enumerate(ts[i : i + BANK // n])]
+                for t, part in parts:
+                    s = 4 * c + t
+                    nc.tensor.matmul_mx(
+                        out=part,
+                        lhsT=w2_codes[:, s * P : (s + 1) * P].bitcast(FP8X4),
+                        lhsT_scale=w2_scales[:, s * P : (s + 1) * P],
+                        rhs=fh_codes[:, cols].bitcast(FP8X4),
+                        rhs_scale=fh_scales[:, cols],
+                        start=True,
+                        stop=True,
                     )
+                for t, part in parts:
+                    s = 4 * c + t
+                    out = planes[(group, c)][:, t, :]
+                    if n < BANK or t % 2 == 0:
+                        nc.scalar.activation(out=out, in_=part, func=FUNC.Relu, bias=b2_cols[:, s : s + 1])
+                    else:
+                        nc.vector.tensor_scalar(
+                            out=out, in0=part, scalar1=b2_cols[:, s : s + 1], scalar2=0.0, op0=ALU.add, op1=ALU.max
+                        )
 
-        def interleave_features(four_agents, c):
-            feat_grouped[(four_agents, c)] = stage.tile([P, BANK, 4], BF16, name="feat_grouped", align_bytes=64)
-            nc.vector.tensor_copy(
-                out=feat_grouped[(four_agents, c)][:].rearrange("p (c i) t -> p c t i", i=4),
-                in_=planes[(four_agents, c)][:].rearrange("p t (c i) -> p c t i", i=4),
+        def interleave_features(group, c, copy):
+            n = AGENT_GROUPS[group][1] * BATCH
+            feat_grouped[(group, c)] = stage.tile([P, n, 4], BF16, name="feat_grouped", align_bytes=64)
+            copy(
+                out=feat_grouped[(group, c)][:].rearrange("p (c i) t -> p c t i", i=4),
+                in_=planes[(group, c)][:].rearrange("p t (c i) -> p c t i", i=4),
             )
 
-        def quantise_features(four_agents, c):
-            cols = slice(four_agents * BANK, (four_agents + 1) * BANK)
+        def quantise_features(group, c):
+            first, count = AGENT_GROUPS[group]
+            cols = slice(first * BATCH, (first + count) * BATCH)
             nc.vector.quantize_mx(
                 out=feat_codes[:, c, cols].bitcast(FP8X4),
                 scales=feat_scales[:, c, cols],
-                in_=feat_grouped[(four_agents, c)][:].rearrange("p c t -> p (c t)"),
+                in_=feat_grouped[(group, c)][:].rearrange("p c t -> p (c t)"),
             )
 
         wih_grouped = {}
@@ -211,16 +235,22 @@ def tile_ppo_actor_pa_kernel(tc, f_hid, h0, c0, W2, b2, W_ih, W_hh, b_ih, b_hh, 
         squashed = {}
         h_c = {}
 
-        def flip_input_weights(n, half, c):
-            if n < AGENTS:
-                wih_grouped[(n, half, c)] = flip_unit(pair_words(wih_raw[(n, half)]), c * PASS_WORDS, [SCALAR, SCALAR])
+        def flip_input_weights(n, half, gate):
+            if gate == 0:
+                wih_grouped[(n, half)] = stage.tile([P, 8 * BANK], BF16, name="wih_grouped", align_bytes=64)
+            words = blocks_of_words(wih_raw[(n, half)], 4)
+            grouped_words = wih_grouped[(n, half)][:].bitcast(F32)
+            for c in range(2):
+                i = 2 * gate + c
+                cols = slice(i * BANK, (i + 1) * BANK)
+                flip_bank(words[:, 2 * gate : 2 * gate + 2, :], c * PASS_WORDS, grouped_words[:, cols], SCALAR)
 
-        def quantise_input_weights(n, half, c):
-            if n == AGENTS:
-                return
-            wih_codes[(n, half, c)] = units.tile([P, BANK], U32, name="wih_codes", align_bytes=64)
-            wih_scales[(n, half, c)] = units.tile([P, BANK], U8, name="wih_scales", align_bytes=64)
-            quantise(wih_codes[(n, half, c)], wih_scales[(n, half, c)], 0, wih_grouped[(n, half, c)])
+        def quantise_input_weights(n, half, which):
+            if which[0] == 0:
+                wih_codes[(n, half)] = units.tile([P, 2 * BANK], U32, name="wih_codes", align_bytes=64)
+                wih_scales[(n, half)] = units.tile([P, 2 * BANK], U8, name="wih_scales", align_bytes=64)
+            values = slice(which[0] * 4 * BANK, (which[-1] + 1) * 4 * BANK)
+            quantise(wih_codes[(n, half)], wih_scales[(n, half)], which[0] * BANK, wih_grouped[(n, half)][:, values])
 
         def flip_recurrent_weights(n, half, copy_out):
             if n == AGENTS:
@@ -231,7 +261,7 @@ def tile_ppo_actor_pa_kernel(tc, f_hid, h0, c0, W2, b2, W_ih, W_hh, b_ih, b_hh, 
             cols = slice(half * BANK, (half + 1) * BANK)
             flip_pairs(words[:, cols], whhT[n][:, cols, :], copy_out)
 
-        def recurrent_group(n, half):
+        def recurrent_group(n, half, copy_out):
             hh_bank = banks.tile([P, BANK], F32, tag="bank")
             if n < BIAS_BY_TRANSPOSE:
                 for i in range(4):
@@ -262,29 +292,33 @@ def tile_ppo_actor_pa_kernel(tc, f_hid, h0, c0, W2, b2, W_ih, W_hh, b_ih, b_hh, 
                     stop=(e == 1),
                 )
             hh_sb[(n, half)] = work.tile([P, BANK], F32, name="hh_sb")
-            nc.vector.tensor_copy(
+            copy_out(
                 out=hh_sb[(n, half)][:].rearrange("b (q p j) -> b q p j", q=2, j=2),
                 in_=hh_bank[:].rearrange("b (q j p) -> b q p j", q=2, j=2),
             )
 
-        def input_group(n, half):
+        def input_group(n, half, which):
             mx_bank = banks.tile([P, BANK], F32, tag="bank")
-            for c in range(2):
-                nc.tensor.matmul_mx(
-                    out=mx_bank[:],
-                    lhsT=feat_codes[:, c, n * BATCH : (n + 1) * BATCH].bitcast(FP8X4),
-                    lhsT_scale=feat_scales[:, c, n * BATCH : (n + 1) * BATCH],
-                    rhs=wih_codes[(n, half, c)][:].bitcast(FP8X4),
-                    rhs_scale=wih_scales[(n, half, c)][:],
-                    start=(c == 0),
-                    stop=(c == 1),
-                )
-            if half == 0:
+            width = len(which) * H
+            for i, gate in enumerate(which):
+                for c in range(2):
+                    cols = slice((2 * gate + c) * H, (2 * gate + c + 1) * H)
+                    nc.tensor.matmul_mx(
+                        out=mx_bank[:, i * H : (i + 1) * H],
+                        lhsT=feat_codes[:, c, n * BATCH : (n + 1) * BATCH].bitcast(FP8X4),
+                        lhsT_scale=feat_scales[:, c, n * BATCH : (n + 1) * BATCH],
+                        rhs=wih_codes[(n, half)][:, cols].bitcast(FP8X4),
+                        rhs_scale=wih_scales[(n, half)][:, cols],
+                        start=(c == 0),
+                        stop=(c == 1),
+                    )
+            if n not in gates:
                 gates[n] = work.tile([P, G], F32, name="gates")
+            first = which[0] * H
             nc.vector.tensor_tensor(
-                out=gates[n][:, half * BANK : (half + 1) * BANK].rearrange("b (q p j) -> b q p j", q=2, j=2),
-                in0=mx_bank[:].rearrange("b (q j p) -> b q p j", q=2, j=2),
-                in1=hh_sb[(n, half)][:].rearrange("b (q p j) -> b q p j", q=2, j=2),
+                out=gates[n][:, half * BANK + first : half * BANK + first + width].rearrange("b (q p j) -> b q p j", p=P, j=2),
+                in0=mx_bank[:, 0:width].rearrange("b (q j p) -> b q p j", p=P, j=2),
+                in1=hh_sb[(n, half)][:, first : first + width].rearrange("b (q p j) -> b q p j", p=P, j=2),
                 op=ALU.add,
             )
 
@@ -296,8 +330,10 @@ def tile_ppo_actor_pa_kernel(tc, f_hid, h0, c0, W2, b2, W_ih, W_hh, b_ih, b_hh, 
         def keep_old_state(n):
             nc.vector.tensor_tensor(out=h_c[n][:, 0, :], in0=squashed[n][:, H : 2 * H], in1=c0_sb[:, n, :], op=ALU.mult)
 
-        def squash_candidate_and_output(n):
+        def squash_candidate(n):
             nc.scalar.activation(out=squashed[n][:, 2 * H : 3 * H], in_=gates[n][:, 2 * H : 3 * H], func=FUNC.Tanh)
+
+        def squash_output_gate(n):
             nc.scalar.activation(out=squashed[n][:, 3 * H : 4 * H], in_=gates[n][:, 3 * H : 4 * H], func=FUNC.Sigmoid)
 
         def new_state(n):
@@ -316,41 +352,43 @@ def tile_ppo_actor_pa_kernel(tc, f_hid, h0, c0, W2, b2, W_ih, W_hh, b_ih, b_hh, 
             nc.vector.tensor_tensor(out=h_c[n][:, 0, :], in0=squashed[n][:, 3 * H : 4 * H], in1=tanh_c[n][:], op=ALU.mult)
             nc.sync.dma_start(out=out_0[n], in_=h_c[n][:, 0, :])
 
-        feature_planes(0, 0, [0, 1, 2, 3])
-        w2_grouped = flip_unit(pair_words(w2_raw[1]), 0, [SCALAR, VECTOR])
-        quantise(w2_codes, w2_scales, 1, w2_grouped)
-        interleave_features(0, 0)
-        feature_planes(0, 1, [0, 1, 2, 3])
+        for c in range(2):
+            feature_planes(0, c, [0, 1, 2, 3])
         flip_input_weights(0, 0, 0)
-        quantise_features(0, 0)
-        interleave_features(0, 1)
+        for c in range(2):
+            interleave_features(0, c, VECTOR)
         flip_input_weights(0, 0, 1)
-        quantise_input_weights(0, 0, 0)
-        quantise_features(0, 1)
+        for c in range(2):
+            quantise_features(0, c)
         h0T = keep.tile([P, AGENTS * BATCH, 2], BF16)
         h0_words = h0_raw[:].rearrange("p n k -> p (n k)").bitcast(F32)
         flip_pairs(h0_words[:, 0:BANK], h0T[:, 0:BANK, :], VECTOR)
         flip_recurrent_weights(0, 0, VECTOR)
+        quantise_input_weights(0, 0, [0, 1])
         flip_recurrent_weights(0, 1, VECTOR)
-        quantise_input_weights(0, 0, 1)
 
-        def feature_work(step, late):
-            if not late:
-                if step == 1:
-                    fh_late.append(flip_unit(pair_words(fh_raw[1]), 0, [SCALAR, VECTOR]))
-                    flip_pairs(h0_words[:, BANK : 2 * BANK], h0T[:, BANK : 2 * BANK, :], VECTOR)
-                return
-            if step == 1:
-                quantise(fh_codes, fh_scales, 1, fh_late[0])
-            elif step in (2, 3, 4, 5):
-                c, second = divmod(step - 2, 2)
-                feature_planes(1, c, [2, 3] if second else [0, 1])
+        def feature_work(step):
+            if step == 0:
+                quantise(fh_codes, fh_scales, 2 * BATCH, flip_rows(fh_raw[2], 2, [SCALAR]))
+            if step in (1, 2):
+                feature_planes(1, step - 1, [0, 1, 2, 3])
+                interleave_features(1, step - 1, GPSIMD)
+            if step in (2, 3):
+                quantise_features(1, step - 2)
+            if step == 2:
+                quantise(fh_codes, fh_scales, 4 * BATCH, flip_rows(fh_raw[4], 4, [SCALAR, VECTOR]))
+            if step == 3:
+                flip_pairs(h0_words[:, BANK : 2 * BANK], h0T[:, BANK : 2 * BANK, :], VECTOR)
+            if step in (3, 4, 5, 6):
+                c, second = divmod(step - 3, 2)
+                feature_planes(2, c, [2, 3] if second else [0, 1])
                 if second:
-                    interleave_features(1, c)
-                    quantise_features(1, c)
+                    interleave_features(2, c, GPSIMD)
+            if step in (6, 7):
+                quantise_features(2, step - 6)
 
-        fh_late = []
-        for step in range(2 * AGENTS):
+        last = AGENTS - 1
+        for step in range(2 * AGENTS - 1):
             n, half = divmod(step, 2)
             m, mhalf = divmod(step + 1, 2)
             flip_input_weights(m, mhalf, 0)
@@ -366,23 +404,32 @@ def tile_ppo_actor_pa_kernel(tc, f_hid, h0, c0, W2, b2, W_ih, W_hh, b_ih, b_hh, 
                     new_output(n - 2)
                 if n > 0:
                     keep_old_state(n - 1)
-                    squash_candidate_and_output(n - 1)
-            recurrent_group(n, half)
-            quantise_input_weights(m, mhalf, 0)
+                    squash_candidate(n - 1)
+                    squash_output_gate(n - 1)
+            recurrent_group(n, half, VECTOR)
+            if n == last:
+                quantise_input_weights(last, 1, [0])
             flip_input_weights(m, mhalf, 1)
             if half == 0 and n + 3 < AGENTS:
                 load_input_weights(n + 3, 1)
-            flip_recurrent_weights(n + 1, half, VECTOR if half else SCALAR)
-            feature_work(step, False)
+            if n < last:
+                flip_recurrent_weights(n + 1, half, VECTOR if half else SCALAR)
             if half == 1 and n > 0:
                 squash_state(n - 1)
-            input_group(n, half)
-            quantise_input_weights(m, mhalf, 1)
-            feature_work(step, True)
-        new_output(AGENTS - 2)
-        keep_old_state(AGENTS - 1)
-        n = AGENTS - 1
-        squash_candidate_and_output(n)
-        new_state(n)
-        squash_state(n)
-        new_output(n)
+            input_group(n, half, [0, 1])
+            feature_work(step)
+            quantise_input_weights(m, mhalf, [1] if n == last else [0, 1])
+
+        squash_input_and_forget(last)
+        recurrent_group(last, 1, SCALAR)
+        input_group(last, 1, [0])
+        squash_candidate(last)
+        new_state(last - 1)
+        squash_state(last - 1)
+        keep_old_state(last)
+        new_state(last)
+        input_group(last, 1, [1])
+        squash_state(last)
+        squash_output_gate(last)
+        new_output(last - 1)
+        new_output(last)

@@ -34,7 +34,7 @@ def tile_ppo_actor_pa_kernel(tc, f_hid, h0, c0, W2, b2, W_ih, W_hh, b_ih, b_hh, 
         tc.tile_pool(name="raw_ih", bufs=6) as raw_ih,
         tc.tile_pool(name="stage", bufs=2) as stage,
         tc.tile_pool(name="units", bufs=3) as units,
-        tc.tile_pool(name="work", bufs=3) as work,
+        tc.tile_pool(name="work", bufs=2) as work,
         tc.psum_pool(name="banks", bufs=8) as banks,
         tc.manual_schedule(),
     ):
@@ -108,7 +108,7 @@ def tile_ppo_actor_pa_kernel(tc, f_hid, h0, c0, W2, b2, W_ih, W_hh, b_ih, b_hh, 
         load_state(c0_sb, c0, 4)
 
         def flip_bank(words, word, grouped_words, copy_out):
-            bank = banks.tile([P, BANK], F32, tag="bank")
+            bank = banks.tile([P, BANK], F32, name="bank")
             for a in range(2):
                 for u in range(2):
                     nc.tensor.transpose(
@@ -121,13 +121,16 @@ def tile_ppo_actor_pa_kernel(tc, f_hid, h0, c0, W2, b2, W_ih, W_hh, b_ih, b_hh, 
                 in_=bank[:].rearrange("p (a u c) -> p a c u", a=2, u=2),
             )
 
-        def flip_pairs(words, pairs, copy_out):
-            bank = banks.tile([P, BANK], F32, tag="bank")
-            for i in range(4):
+        def flip_blocks(bank, words, blocks):
+            for i in blocks:
                 nc.tensor.transpose(bank[:, i * P : (i + 1) * P], words[:, i * P : (i + 1) * P], identity[:])
+
+        def flip_pairs(words, pairs, copy_out):
+            bank = banks.tile([P, BANK], F32, name="bank")
+            flip_blocks(bank, words, range(4))
             copy_out(out=pairs.rearrange("p c e -> p (c e)"), in_=bank[:].bitcast(BF16))
 
-        SCALAR, VECTOR, GPSIMD = nc.scalar.copy, nc.vector.tensor_copy, nc.gpsimd.tensor_copy
+        SCALAR, VECTOR = nc.scalar.copy, nc.vector.tensor_copy
 
         fh_codes = keep.tile([P, AGENTS * BATCH], U32, align_bytes=64)
         fh_scales = keep.tile([P, AGENTS * BATCH], U8, align_bytes=64)
@@ -156,7 +159,7 @@ def tile_ppo_actor_pa_kernel(tc, f_hid, h0, c0, W2, b2, W_ih, W_hh, b_ih, b_hh, 
         w2_grouped.append(flip_rows(w2_raw[1], 4, [SCALAR, VECTOR]))
         quantise(w2_codes, w2_scales, 0, w2_grouped[0])
 
-        vec_bank = banks.tile([P, BANK], F32, tag="bank")
+        vec_bank = banks.tile([P, BANK], F32, name="bank")
         nc.tensor.transpose(vec_bank[:, 0:P], vec_rows[:].bitcast(F32), identity[:])
         for u in range(2):
             nc.tensor.transpose(
@@ -186,7 +189,7 @@ def tile_ppo_actor_pa_kernel(tc, f_hid, h0, c0, W2, b2, W_ih, W_hh, b_ih, b_hh, 
             if ts[0] == 0:
                 planes[(group, c)] = stage.tile([P, 4, n], BF16, name="planes")
             for i in range(0, len(ts), BANK // n):
-                f_bank = banks.tile([P, BANK], F32, tag="bank")
+                f_bank = banks.tile([P, BANK], F32, name="bank")
                 parts = [(t, f_bank[:, k * n : (k + 1) * n]) for k, t in enumerate(ts[i : i + BANK // n])]
                 for t, part in parts:
                     s = 4 * c + t
@@ -202,17 +205,12 @@ def tile_ppo_actor_pa_kernel(tc, f_hid, h0, c0, W2, b2, W_ih, W_hh, b_ih, b_hh, 
                 for t, part in parts:
                     s = 4 * c + t
                     out = planes[(group, c)][:, t, :]
-                    if n < BANK or t % 2 == 0:
-                        nc.scalar.activation(out=out, in_=part, func=FUNC.Relu, bias=b2_cols[:, s : s + 1])
-                    else:
-                        nc.vector.tensor_scalar(
-                            out=out, in0=part, scalar1=b2_cols[:, s : s + 1], scalar2=0.0, op0=ALU.add, op1=ALU.max
-                        )
+                    nc.scalar.activation(out=out, in_=part, func=FUNC.Relu, bias=b2_cols[:, s : s + 1])
 
-        def interleave_features(group, c, copy):
+        def interleave_features(group, c):
             n = AGENT_GROUPS[group][1] * BATCH
             feat_grouped[(group, c)] = stage.tile([P, n, 4], BF16, name="feat_grouped", align_bytes=64)
-            copy(
+            nc.vector.tensor_copy(
                 out=feat_grouped[(group, c)][:].rearrange("p (c i) t -> p c t i", i=4),
                 in_=planes[(group, c)][:].rearrange("p t (c i) -> p c t i", i=4),
             )
@@ -229,11 +227,15 @@ def tile_ppo_actor_pa_kernel(tc, f_hid, h0, c0, W2, b2, W_ih, W_hh, b_ih, b_hh, 
         wih_grouped = {}
         wih_codes = {}
         wih_scales = {}
+        whh_banks = {}
         whhT = {}
         hh_sb = {}
         gates = {}
         squashed = {}
         h_c = {}
+
+        def code_block(n, half, gate, c):
+            return 2 * gate + c if (n, half) == (AGENTS - 1, 1) else 2 * c + gate
 
         def flip_input_weights(n, half, gate):
             if gate == 0:
@@ -241,7 +243,7 @@ def tile_ppo_actor_pa_kernel(tc, f_hid, h0, c0, W2, b2, W_ih, W_hh, b_ih, b_hh, 
             words = blocks_of_words(wih_raw[(n, half)], 4)
             grouped_words = wih_grouped[(n, half)][:].bitcast(F32)
             for c in range(2):
-                i = 2 * gate + c
+                i = code_block(n, half, gate, c)
                 cols = slice(i * BANK, (i + 1) * BANK)
                 flip_bank(words[:, 2 * gate : 2 * gate + 2, :], c * PASS_WORDS, grouped_words[:, cols], SCALAR)
 
@@ -252,17 +254,20 @@ def tile_ppo_actor_pa_kernel(tc, f_hid, h0, c0, W2, b2, W_ih, W_hh, b_ih, b_hh, 
             values = slice(which[0] * 4 * BANK, (which[-1] + 1) * 4 * BANK)
             quantise(wih_codes[(n, half)], wih_scales[(n, half)], which[0] * BANK, wih_grouped[(n, half)][:, values])
 
-        def flip_recurrent_weights(n, half, copy_out):
-            if n == AGENTS:
-                return
-            if half == 0:
-                whhT[n] = work.tile([P, G, 2], BF16, name="whhT")
+        def flip_recurrent_weights(n, half, blocks):
+            if (n, half) not in whh_banks:
+                whh_banks[(n, half)] = banks.tile([P, BANK], F32, name="bank")
             words = whh_raw[n][:].rearrange("p q k -> p (q k)").bitcast(F32)
-            cols = slice(half * BANK, (half + 1) * BANK)
-            flip_pairs(words[:, cols], whhT[n][:, cols, :], copy_out)
+            flip_blocks(whh_banks[(n, half)], words[:, half * BANK : (half + 1) * BANK], blocks)
+
+        def empty_recurrent_weights(n, half, copy_out):
+            if n not in whhT:
+                whhT[n] = work.tile([P, G, 2], BF16, name="whhT")
+            pairs = whhT[n][:, half * BANK : (half + 1) * BANK, :]
+            copy_out(out=pairs.rearrange("p c e -> p (c e)"), in_=whh_banks[(n, half)][:].bitcast(BF16))
 
         def recurrent_group(n, half, copy_out):
-            hh_bank = banks.tile([P, BANK], F32, tag="bank")
+            hh_bank = banks.tile([P, BANK], F32, name="bank")
             if n < BIAS_BY_TRANSPOSE:
                 for i in range(4):
                     m = 8 * n + 4 * half + i
@@ -298,20 +303,20 @@ def tile_ppo_actor_pa_kernel(tc, f_hid, h0, c0, W2, b2, W_ih, W_hh, b_ih, b_hh, 
             )
 
         def input_group(n, half, which):
-            mx_bank = banks.tile([P, BANK], F32, tag="bank")
+            mx_bank = banks.tile([P, BANK], F32, name="bank")
             width = len(which) * H
-            for i, gate in enumerate(which):
-                for c in range(2):
-                    cols = slice((2 * gate + c) * H, (2 * gate + c + 1) * H)
-                    nc.tensor.matmul_mx(
-                        out=mx_bank[:, i * H : (i + 1) * H],
-                        lhsT=feat_codes[:, c, n * BATCH : (n + 1) * BATCH].bitcast(FP8X4),
-                        lhsT_scale=feat_scales[:, c, n * BATCH : (n + 1) * BATCH],
-                        rhs=wih_codes[(n, half)][:, cols].bitcast(FP8X4),
-                        rhs_scale=wih_scales[(n, half)][:, cols],
-                        start=(c == 0),
-                        stop=(c == 1),
-                    )
+            for c in range(2):
+                block = code_block(n, half, which[0], c)
+                cols = slice(block * H, block * H + width)
+                nc.tensor.matmul_mx(
+                    out=mx_bank[:, 0:width],
+                    lhsT=feat_codes[:, c, n * BATCH : (n + 1) * BATCH].bitcast(FP8X4),
+                    lhsT_scale=feat_scales[:, c, n * BATCH : (n + 1) * BATCH],
+                    rhs=wih_codes[(n, half)][:, cols].bitcast(FP8X4),
+                    rhs_scale=wih_scales[(n, half)][:, cols],
+                    start=(c == 0),
+                    stop=(c == 1),
+                )
             if n not in gates:
                 gates[n] = work.tile([P, G], F32, name="gates")
             first = which[0] * H
@@ -356,25 +361,24 @@ def tile_ppo_actor_pa_kernel(tc, f_hid, h0, c0, W2, b2, W_ih, W_hh, b_ih, b_hh, 
             feature_planes(0, c, [0, 1, 2, 3])
         flip_input_weights(0, 0, 0)
         for c in range(2):
-            interleave_features(0, c, VECTOR)
+            interleave_features(0, c)
         flip_input_weights(0, 0, 1)
         for c in range(2):
             quantise_features(0, c)
         h0T = keep.tile([P, AGENTS * BATCH, 2], BF16)
         h0_words = h0_raw[:].rearrange("p n k -> p (n k)").bitcast(F32)
         flip_pairs(h0_words[:, 0:BANK], h0T[:, 0:BANK, :], VECTOR)
-        flip_recurrent_weights(0, 0, VECTOR)
+        flip_recurrent_weights(0, 0, range(4))
+        empty_recurrent_weights(0, 0, VECTOR)
         quantise_input_weights(0, 0, [0, 1])
-        flip_recurrent_weights(0, 1, VECTOR)
+        flip_recurrent_weights(0, 1, range(4))
+        empty_recurrent_weights(0, 1, VECTOR)
 
         def feature_work(step):
             if step == 0:
                 quantise(fh_codes, fh_scales, 2 * BATCH, flip_rows(fh_raw[2], 2, [SCALAR]))
             if step in (1, 2):
                 feature_planes(1, step - 1, [0, 1, 2, 3])
-                interleave_features(1, step - 1, GPSIMD)
-            if step in (2, 3):
-                quantise_features(1, step - 2)
             if step == 2:
                 quantise(fh_codes, fh_scales, 4 * BATCH, flip_rows(fh_raw[4], 4, [SCALAR, VECTOR]))
             if step == 3:
@@ -382,16 +386,24 @@ def tile_ppo_actor_pa_kernel(tc, f_hid, h0, c0, W2, b2, W_ih, W_hh, b_ih, b_hh, 
             if step in (3, 4, 5, 6):
                 c, second = divmod(step - 3, 2)
                 feature_planes(2, c, [2, 3] if second else [0, 1])
-                if second:
-                    interleave_features(2, c, GPSIMD)
-            if step in (6, 7):
-                quantise_features(2, step - 6)
+
+        def feature_copies(step):
+            for group, c, first_step in ((1, 0, 2), (1, 1, 3), (2, 0, 5), (2, 1, 7)):
+                if step == first_step:
+                    interleave_features(group, c)
+
+        def feature_codings(step):
+            for group, c, first_step in ((1, 0, 2), (1, 1, 3), (2, 0, 5), (2, 1, 7)):
+                if step == first_step:
+                    quantise_features(group, c)
 
         last = AGENTS - 1
         for step in range(2 * AGENTS - 1):
             n, half = divmod(step, 2)
             m, mhalf = divmod(step + 1, 2)
             flip_input_weights(m, mhalf, 0)
+            if n < last:
+                flip_recurrent_weights(n + 1, half, range(2))
             if half == 0 and n + 3 < AGENTS:
                 load_input_weights(n + 3, 0)
                 load_recurrent_weights(n + 3)
@@ -406,6 +418,7 @@ def tile_ppo_actor_pa_kernel(tc, f_hid, h0, c0, W2, b2, W_ih, W_hh, b_ih, b_hh, 
                     keep_old_state(n - 1)
                     squash_candidate(n - 1)
                     squash_output_gate(n - 1)
+            feature_copies(step)
             recurrent_group(n, half, VECTOR)
             if n == last:
                 quantise_input_weights(last, 1, [0])
@@ -413,9 +426,11 @@ def tile_ppo_actor_pa_kernel(tc, f_hid, h0, c0, W2, b2, W_ih, W_hh, b_ih, b_hh, 
             if half == 0 and n + 3 < AGENTS:
                 load_input_weights(n + 3, 1)
             if n < last:
-                flip_recurrent_weights(n + 1, half, VECTOR if half else SCALAR)
+                flip_recurrent_weights(n + 1, half, range(2, 4))
+                empty_recurrent_weights(n + 1, half, VECTOR if half else SCALAR)
             if half == 1 and n > 0:
                 squash_state(n - 1)
+            feature_codings(step)
             input_group(n, half, [0, 1])
             feature_work(step)
             quantise_input_weights(m, mhalf, [1] if n == last else [0, 1])

@@ -21,7 +21,6 @@ PASS_WORDS = 256
 
 BIAS_BY_TRANSPOSE = 2
 
-AGENT_GROUPS = ((0, 2), (2, 2), (4, 4))
 
 FLOPS = 2 * BATCH * AGENTS * (M1 * F + F * G + H * G)
 
@@ -57,7 +56,7 @@ def tile_ppo_actor_pa_kernel(tc, f_hid, h0, c0, W2, b2, W_ih, W_hh, b_ih, b_hh, 
             whh_raw[n] = raw_hh.tile([P, 4, 2 * H], BF16, name="whh_raw")
             nc.sync.dma_start(out=whh_raw[n][:], in_=W_hh[n].rearrange("(q p j) k -> p q (j k)", p=P, j=2))
 
-        fh_raw = {first: keep.tile([P, count, M1], BF16, name="fh_raw%d" % first) for first, count in AGENT_GROUPS}
+        fh_raw = {first: keep.tile([P, 2, M1], BF16, name="fh_raw%d" % first) for first in range(0, AGENTS, 2)}
         w2_raw = [keep.tile([P, 4, M1], BF16, name="w2_raw%d" % c) for c in range(2)]
         vec_rows = keep.tile([P, 2 * P], BF16)
         nc.vector.memset(vec_rows[:].bitcast(F32), 0.0)
@@ -71,8 +70,8 @@ def tile_ppo_actor_pa_kernel(tc, f_hid, h0, c0, W2, b2, W_ih, W_hh, b_ih, b_hh, 
         ones = keep.tile([P, P], BF16)
         nc.gpsimd.memset(ones[:], 1.0)
 
-        def load_f_hid(first, count):
-            nc.sync.dma_start(out=fh_raw[first][:], in_=f_hid[:, first : first + count, :])
+        def load_f_hid(first):
+            nc.sync.dma_start(out=fh_raw[first][:], in_=f_hid[:, first : first + 2, :])
 
         def load_state(tile, state, first):
             agents = slice(first, first + 4)
@@ -81,7 +80,7 @@ def tile_ppo_actor_pa_kernel(tc, f_hid, h0, c0, W2, b2, W_ih, W_hh, b_ih, b_hh, 
         def load_feature_weights(c):
             nc.sync.dma_start(out=w2_raw[c][:], in_=W2[c * BANK : (c + 1) * BANK, :].rearrange("(p t) k -> p t k", t=4))
 
-        load_f_hid(*AGENT_GROUPS[0])
+        load_f_hid(0)
         load_feature_weights(0)
         nc.sync.dma_start(out=b2_rows[0:2, :], in_=b2.rearrange("(c w) -> c w", w=4 * P))
         nc.sync.dma_start(out=vec_rows[0:32, :], in_=b_ih.rearrange("n (q w) -> (n q) w", w=2 * P))
@@ -91,7 +90,7 @@ def tile_ppo_actor_pa_kernel(tc, f_hid, h0, c0, W2, b2, W_ih, W_hh, b_ih, b_hh, 
         load_state(h0_raw, h0, 0)
         load_recurrent_weights(0)
         load_input_weights(0, 1)
-        load_f_hid(*AGENT_GROUPS[1])
+        load_f_hid(2)
         load_recurrent_weights(1)
         load_input_weights(1, 0)
         load_state(c0_sb, c0, 0)
@@ -101,7 +100,8 @@ def tile_ppo_actor_pa_kernel(tc, f_hid, h0, c0, W2, b2, W_ih, W_hh, b_ih, b_hh, 
             )
         load_input_weights(1, 1)
         load_recurrent_weights(2)
-        load_f_hid(*AGENT_GROUPS[2])
+        load_f_hid(4)
+        load_f_hid(6)
         load_state(h0_raw, h0, 4)
         load_input_weights(2, 0)
         load_input_weights(2, 1)
@@ -153,9 +153,9 @@ def tile_ppo_actor_pa_kernel(tc, f_hid, h0, c0, W2, b2, W_ih, W_hh, b_ih, b_hh, 
                 flip_bank(words[:, 2 * i : 2 * i + 2, :], 0, grouped_words[:, cols], copy_outs[i])
             return grouped[:]
 
-        fh_grouped = flip_rows(fh_raw[0], 2, [SCALAR])
+        fh_grouped = {0: flip_rows(fh_raw[0], 2, [SCALAR])}
         w2_grouped = [flip_rows(w2_raw[0], 4, [SCALAR, SCALAR])]
-        quantise(fh_codes, fh_scales, 0, fh_grouped)
+        quantise(fh_codes, fh_scales, 0, fh_grouped[0])
         w2_grouped.append(flip_rows(w2_raw[1], 4, [SCALAR, VECTOR]))
         quantise(w2_codes, w2_scales, 0, w2_grouped[0])
 
@@ -177,52 +177,45 @@ def tile_ppo_actor_pa_kernel(tc, f_hid, h0, c0, W2, b2, W_ih, W_hh, b_ih, b_hh, 
         gate_bias = keep.tile([P, 64], F32)
         nc.vector.tensor_tensor(out=gate_bias[:], in0=vec_cols[:, 0:64], in1=vec_cols[:, 64:128], op=ALU.add)
 
-        feat_codes = keep.tile([P, 2, AGENTS * BATCH], U32, align_bytes=64)
-        feat_scales = keep.tile([P, 2, AGENTS * BATCH], U8, align_bytes=64)
-        planes = {}
-        feat_grouped = {}
+        feat_banks = {}
+        feat_sums = {}
+        feat_codes = {}
+        feat_scales = {}
 
-        def feature_planes(group, c, ts):
-            first, count = AGENT_GROUPS[group]
-            n = count * BATCH
-            cols = slice(first * BATCH, first * BATCH + n)
-            if ts[0] == 0:
-                planes[(group, c)] = stage.tile([P, 4, n], BF16, name="planes")
-            for i in range(0, len(ts), BANK // n):
-                f_bank = banks.tile([P, BANK], F32, name="bank")
-                parts = [(t, f_bank[:, k * n : (k + 1) * n]) for k, t in enumerate(ts[i : i + BANK // n])]
-                for t, part in parts:
-                    s = 4 * c + t
-                    nc.tensor.matmul_mx(
-                        out=part,
-                        lhsT=w2_codes[:, s * P : (s + 1) * P].bitcast(FP8X4),
-                        lhsT_scale=w2_scales[:, s * P : (s + 1) * P],
-                        rhs=fh_codes[:, cols].bitcast(FP8X4),
-                        rhs_scale=fh_scales[:, cols],
-                        start=True,
-                        stop=True,
-                    )
-                for t, part in parts:
-                    s = 4 * c + t
-                    out = planes[(group, c)][:, t, :]
-                    nc.scalar.activation(out=out, in_=part, func=FUNC.Relu, bias=b2_cols[:, s : s + 1])
+        def make_features(n, c):
+            f_bank = banks.tile([P, BANK], F32, name="bank")
+            cols = slice(n * BATCH, (n + 1) * BATCH)
+            for t in range(4):
+                s = 4 * c + t
+                nc.tensor.matmul_mx(
+                    out=f_bank[:, t * BATCH : (t + 1) * BATCH],
+                    lhsT=w2_codes[:, s * P : (s + 1) * P].bitcast(FP8X4),
+                    lhsT_scale=w2_scales[:, s * P : (s + 1) * P],
+                    rhs=fh_codes[:, cols].bitcast(FP8X4),
+                    rhs_scale=fh_scales[:, cols],
+                    start=True,
+                    stop=True,
+                )
+            feat_banks[(n, c)] = f_bank
 
-        def interleave_features(group, c):
-            n = AGENT_GROUPS[group][1] * BATCH
-            feat_grouped[(group, c)] = stage.tile([P, n, 4], BF16, name="feat_grouped", align_bytes=64)
-            nc.vector.tensor_copy(
-                out=feat_grouped[(group, c)][:].rearrange("p (c i) t -> p c t i", i=4),
-                in_=planes[(group, c)][:].rearrange("p t (c i) -> p c t i", i=4),
+        def add_feature_bias(n, c):
+            if c == 0:
+                feat_sums[n] = stage.tile([P, 2, BATCH, 4], BF16, name="feat_sums", align_bytes=64)
+            nc.vector.tensor_tensor(
+                out=feat_sums[n][:, c, :, :],
+                in0=feat_banks[(n, c)][:].rearrange("p (t b) -> p b t", t=4),
+                in1=b2_cols[:, 4 * c : 4 * c + 4].unsqueeze(1).broadcast_to([P, BATCH, 4]),
+                op=ALU.add,
             )
 
-        def quantise_features(group, c):
-            first, count = AGENT_GROUPS[group]
-            cols = slice(first * BATCH, (first + count) * BATCH)
-            nc.vector.quantize_mx(
-                out=feat_codes[:, c, cols].bitcast(FP8X4),
-                scales=feat_scales[:, c, cols],
-                in_=feat_grouped[(group, c)][:].rearrange("p c t -> p (c t)"),
-            )
+        def rectify_features(n):
+            values = feat_sums[n][:].rearrange("p c b t -> p (c b t)")
+            nc.vector.tensor_scalar_max(out=values, in0=values, scalar1=0.0)
+
+        def quantise_features(n):
+            feat_codes[n] = units.tile([P, 2 * BATCH], U32, name="feat_codes", align_bytes=64)
+            feat_scales[n] = units.tile([P, 2 * BATCH], U8, name="feat_scales", align_bytes=64)
+            quantise(feat_codes[n], feat_scales[n], 0, feat_sums[n][:].rearrange("p c b t -> p (c b t)"))
 
         wih_grouped = {}
         wih_codes = {}
@@ -310,8 +303,8 @@ def tile_ppo_actor_pa_kernel(tc, f_hid, h0, c0, W2, b2, W_ih, W_hh, b_ih, b_hh, 
                 cols = slice(block * H, block * H + width)
                 nc.tensor.matmul_mx(
                     out=mx_bank[:, 0:width],
-                    lhsT=feat_codes[:, c, n * BATCH : (n + 1) * BATCH].bitcast(FP8X4),
-                    lhsT_scale=feat_scales[:, c, n * BATCH : (n + 1) * BATCH],
+                    lhsT=feat_codes[n][:, c * BATCH : (c + 1) * BATCH].bitcast(FP8X4),
+                    lhsT_scale=feat_scales[n][:, c * BATCH : (c + 1) * BATCH],
                     rhs=wih_codes[(n, half)][:, cols].bitcast(FP8X4),
                     rhs_scale=wih_scales[(n, half)][:, cols],
                     start=(c == 0),
@@ -357,45 +350,27 @@ def tile_ppo_actor_pa_kernel(tc, f_hid, h0, c0, W2, b2, W_ih, W_hh, b_ih, b_hh, 
             nc.vector.tensor_tensor(out=h_c[n][:, 0, :], in0=squashed[n][:, 3 * H : 4 * H], in1=tanh_c[n][:], op=ALU.mult)
             nc.sync.dma_start(out=out_0[n], in_=h_c[n][:, 0, :])
 
-        for c in range(2):
-            feature_planes(0, c, [0, 1, 2, 3])
+        for n in range(2):
+            for c in range(2):
+                make_features(n, c)
         flip_input_weights(0, 0, 0)
-        for c in range(2):
-            interleave_features(0, c)
+        for n in range(2):
+            for c in range(2):
+                add_feature_bias(n, c)
+            rectify_features(n)
         flip_input_weights(0, 0, 1)
-        for c in range(2):
-            quantise_features(0, c)
+        quantise_features(0)
+        fh_grouped[2] = flip_rows(fh_raw[2], 2, [SCALAR])
         h0T = keep.tile([P, AGENTS * BATCH, 2], BF16)
         h0_words = h0_raw[:].rearrange("p n k -> p (n k)").bitcast(F32)
         flip_pairs(h0_words[:, 0:BANK], h0T[:, 0:BANK, :], VECTOR)
         flip_recurrent_weights(0, 0, range(4))
         empty_recurrent_weights(0, 0, VECTOR)
         quantise_input_weights(0, 0, [0, 1])
+        quantise(fh_codes, fh_scales, 2 * BATCH, fh_grouped[2])
+        quantise_features(1)
         flip_recurrent_weights(0, 1, range(4))
         empty_recurrent_weights(0, 1, VECTOR)
-
-        def feature_work(step):
-            if step == 0:
-                quantise(fh_codes, fh_scales, 2 * BATCH, flip_rows(fh_raw[2], 2, [SCALAR]))
-            if step in (1, 2):
-                feature_planes(1, step - 1, [0, 1, 2, 3])
-            if step == 2:
-                quantise(fh_codes, fh_scales, 4 * BATCH, flip_rows(fh_raw[4], 4, [SCALAR, VECTOR]))
-            if step == 3:
-                flip_pairs(h0_words[:, BANK : 2 * BANK], h0T[:, BANK : 2 * BANK, :], VECTOR)
-            if step in (3, 4, 5, 6):
-                c, second = divmod(step - 3, 2)
-                feature_planes(2, c, [2, 3] if second else [0, 1])
-
-        def feature_copies(step):
-            for group, c, first_step in ((1, 0, 2), (1, 1, 3), (2, 0, 5), (2, 1, 7)):
-                if step == first_step:
-                    interleave_features(group, c)
-
-        def feature_codings(step):
-            for group, c, first_step in ((1, 0, 2), (1, 1, 3), (2, 0, 5), (2, 1, 7)):
-                if step == first_step:
-                    quantise_features(group, c)
 
         last = AGENTS - 1
         for step in range(2 * AGENTS - 1):
@@ -418,22 +393,33 @@ def tile_ppo_actor_pa_kernel(tc, f_hid, h0, c0, W2, b2, W_ih, W_hh, b_ih, b_hh, 
                     keep_old_state(n - 1)
                     squash_candidate(n - 1)
                     squash_output_gate(n - 1)
-            feature_copies(step)
-            recurrent_group(n, half, VECTOR)
+            if half == 0 and 0 < n < last:
+                rectify_features(n + 1)
+            if n in (1, 3) and half == 1:
+                quantise(fh_codes, fh_scales, (n + 3) * BATCH, fh_grouped[n + 3])
+            recurrent_group(n, half, SCALAR if half else VECTOR)
             if n == last:
                 quantise_input_weights(last, 1, [0])
             flip_input_weights(m, mhalf, 1)
             if half == 0 and n + 3 < AGENTS:
                 load_input_weights(n + 3, 1)
+            if n in (1, 3) and half == 0:
+                fh_grouped[n + 3] = flip_rows(fh_raw[n + 3], 2, [SCALAR])
+            if step == 4:
+                flip_pairs(h0_words[:, BANK : 2 * BANK], h0T[:, BANK : 2 * BANK, :], VECTOR)
             if n < last:
                 flip_recurrent_weights(n + 1, half, range(2, 4))
                 empty_recurrent_weights(n + 1, half, VECTOR if half else SCALAR)
             if half == 1 and n > 0:
                 squash_state(n - 1)
-            feature_codings(step)
+            if half == 0 and 0 < n < last:
+                quantise_features(n + 1)
             input_group(n, half, [0, 1])
-            feature_work(step)
+            if n + 2 < AGENTS:
+                make_features(n + 2, half)
             quantise_input_weights(m, mhalf, [1] if n == last else [0, 1])
+            if n + 2 < AGENTS:
+                add_feature_bias(n + 2, half)
 
         squash_input_and_forget(last)
         recurrent_group(last, 1, SCALAR)

@@ -223,6 +223,7 @@ def tile_ppo_actor_pa_kernel(tc, f_hid, h0, c0, W2, b2, W_ih, W_hh, b_ih, b_hh, 
         whh_banks = {}
         whhT = {}
         hh_sb = {}
+        mx_banks = {}
         gates = {}
         squashed = {}
         h_c = {}
@@ -259,8 +260,11 @@ def tile_ppo_actor_pa_kernel(tc, f_hid, h0, c0, W2, b2, W_ih, W_hh, b_ih, b_hh, 
             pairs = whhT[n][:, half * BANK : (half + 1) * BANK, :]
             copy_out(out=pairs.rearrange("p c e -> p (c e)"), in_=whh_banks[(n, half)][:].bitcast(BF16))
 
-        def recurrent_group(n, half, copy_out):
+        hh_banks = {}
+
+        def open_recurrent_group(n, half):
             hh_bank = banks.tile([P, BANK], F32, name="bank")
+            hh_banks[(n, half)] = hh_bank
             if n < BIAS_BY_TRANSPOSE:
                 for i in range(4):
                     m = 8 * n + 4 * half + i
@@ -281,22 +285,25 @@ def tile_ppo_actor_pa_kernel(tc, f_hid, h0, c0, W2, b2, W_ih, W_hh, b_ih, b_hh, 
                     start=True,
                     stop=False,
                 )
-            for e in range(2):
-                nc.tensor.matmul(
-                    out=hh_bank[:],
-                    lhsT=h0T[:, n * BATCH : (n + 1) * BATCH, e],
-                    rhs=whhT[n][:, half * BANK : (half + 1) * BANK, e],
-                    start=False,
-                    stop=(e == 1),
-                )
+        def add_recurrent_pass(n, half, e):
+            nc.tensor.matmul(
+                out=hh_banks[(n, half)][:],
+                lhsT=h0T[:, n * BATCH : (n + 1) * BATCH, e],
+                rhs=whhT[n][:, half * BANK : (half + 1) * BANK, e],
+                start=False,
+                stop=(e == 1),
+            )
+
+        def empty_recurrent_group(n, half, copy_out):
             hh_sb[(n, half)] = work.tile([P, BANK], F32, name="hh_sb")
             copy_out(
                 out=hh_sb[(n, half)][:].rearrange("b (q p j) -> b q p j", q=2, j=2),
-                in_=hh_bank[:].rearrange("b (q j p) -> b q p j", q=2, j=2),
+                in_=hh_banks[(n, half)][:].rearrange("b (q j p) -> b q p j", q=2, j=2),
             )
 
         def input_group(n, half, which):
             mx_bank = banks.tile([P, BANK], F32, name="bank")
+            mx_banks[(n, half, which[0])] = mx_bank
             width = len(which) * H
             for c in range(2):
                 block = code_block(n, half, which[0], c)
@@ -310,6 +317,10 @@ def tile_ppo_actor_pa_kernel(tc, f_hid, h0, c0, W2, b2, W_ih, W_hh, b_ih, b_hh, 
                     start=(c == 0),
                     stop=(c == 1),
                 )
+
+        def add_groups(n, half, which):
+            width = len(which) * H
+            mx_bank = mx_banks[(n, half, which[0])]
             if n not in gates:
                 gates[n] = work.tile([P, G], F32, name="gates")
             first = which[0] * H
@@ -350,10 +361,10 @@ def tile_ppo_actor_pa_kernel(tc, f_hid, h0, c0, W2, b2, W_ih, W_hh, b_ih, b_hh, 
             nc.vector.tensor_tensor(out=h_c[n][:, 0, :], in0=squashed[n][:, 3 * H : 4 * H], in1=tanh_c[n][:], op=ALU.mult)
             nc.sync.dma_start(out=out_0[n], in_=h_c[n][:, 0, :])
 
+        flip_input_weights(0, 0, 0)
         for n in range(2):
             for c in range(2):
                 make_features(n, c)
-        flip_input_weights(0, 0, 0)
         for n in range(2):
             for c in range(2):
                 add_feature_bias(n, c)
@@ -371,6 +382,10 @@ def tile_ppo_actor_pa_kernel(tc, f_hid, h0, c0, W2, b2, W_ih, W_hh, b_ih, b_hh, 
         quantise_features(1)
         flip_recurrent_weights(0, 1, range(4))
         empty_recurrent_weights(0, 1, VECTOR)
+        open_recurrent_group(0, 0)
+        for e in range(2):
+            add_recurrent_pass(0, 0, e)
+        empty_recurrent_group(0, 0, VECTOR)
 
         last = AGENTS - 1
         for step in range(2 * AGENTS - 1):
@@ -397,7 +412,7 @@ def tile_ppo_actor_pa_kernel(tc, f_hid, h0, c0, W2, b2, W_ih, W_hh, b_ih, b_hh, 
                 rectify_features(n + 1)
             if n in (1, 3) and half == 1:
                 quantise(fh_codes, fh_scales, (n + 3) * BATCH, fh_grouped[n + 3])
-            recurrent_group(n, half, SCALAR if half else VECTOR)
+            open_recurrent_group(m, mhalf)
             if n == last:
                 quantise_input_weights(last, 1, [0])
             flip_input_weights(m, mhalf, 1)
@@ -414,22 +429,27 @@ def tile_ppo_actor_pa_kernel(tc, f_hid, h0, c0, W2, b2, W_ih, W_hh, b_ih, b_hh, 
                 squash_state(n - 1)
             if half == 0 and 0 < n < last:
                 quantise_features(n + 1)
+            add_recurrent_pass(m, mhalf, 0)
             input_group(n, half, [0, 1])
             if n + 2 < AGENTS:
                 make_features(n + 2, half)
+            add_recurrent_pass(m, mhalf, 1)
+            add_groups(n, half, [0, 1])
+            empty_recurrent_group(m, mhalf, SCALAR)
             quantise_input_weights(m, mhalf, [1] if n == last else [0, 1])
             if n + 2 < AGENTS:
                 add_feature_bias(n + 2, half)
 
         squash_input_and_forget(last)
-        recurrent_group(last, 1, SCALAR)
         input_group(last, 1, [0])
+        add_groups(last, 1, [0])
         squash_candidate(last)
         new_state(last - 1)
         squash_state(last - 1)
         keep_old_state(last)
         new_state(last)
         input_group(last, 1, [1])
+        add_groups(last, 1, [1])
         squash_state(last)
         squash_output_gate(last)
         new_output(last - 1)

@@ -128,7 +128,7 @@ def tile_ppo_actor_pa_kernel(tc, f_hid, h0, c0, W2, b2, W_ih, W_hh, b_ih, b_hh, 
         def flip_pairs(words, pairs, copy_out):
             bank = banks.tile([P, BANK], F32, name="bank")
             flip_blocks(bank, words, range(4))
-            copy_out(out=pairs.rearrange("p c e -> p (c e)"), in_=bank[:].bitcast(BF16))
+            copy_out(out=pairs.rearrange("p c e -> p (c e)").bitcast(F32), in_=bank[:])
 
         SCALAR, VECTOR = nc.scalar.copy, nc.vector.tensor_copy
 
@@ -258,7 +258,7 @@ def tile_ppo_actor_pa_kernel(tc, f_hid, h0, c0, W2, b2, W_ih, W_hh, b_ih, b_hh, 
             if n not in whhT:
                 whhT[n] = work.tile([P, G, 2], BF16, name="whhT")
             pairs = whhT[n][:, half * BANK : (half + 1) * BANK, :]
-            copy_out(out=pairs.rearrange("p c e -> p (c e)"), in_=whh_banks[(n, half)][:].bitcast(BF16))
+            copy_out(out=pairs.rearrange("p c e -> p (c e)").bitcast(F32), in_=whh_banks[(n, half)][:])
 
         hh_banks = {}
 
@@ -370,22 +370,22 @@ def tile_ppo_actor_pa_kernel(tc, f_hid, h0, c0, W2, b2, W_ih, W_hh, b_ih, b_hh, 
                 add_feature_bias(n, c)
             rectify_features(n)
         flip_input_weights(0, 0, 1)
-        quantise_features(0)
-        fh_grouped[2] = flip_rows(fh_raw[2], 2, [SCALAR])
         h0T = keep.tile([P, AGENTS * BATCH, 2], BF16)
         h0_words = h0_raw[:].rearrange("p n k -> p (n k)").bitcast(F32)
-        flip_pairs(h0_words[:, 0:BANK], h0T[:, 0:BANK, :], VECTOR)
+        flip_pairs(h0_words[:, 0:BANK], h0T[:, 0:BANK, :], SCALAR)
         flip_recurrent_weights(0, 0, range(4))
-        empty_recurrent_weights(0, 0, VECTOR)
-        quantise_input_weights(0, 0, [0, 1])
-        quantise(fh_codes, fh_scales, 2 * BATCH, fh_grouped[2])
-        quantise_features(1)
+        empty_recurrent_weights(0, 0, SCALAR)
+        quantise_features(0)
         flip_recurrent_weights(0, 1, range(4))
-        empty_recurrent_weights(0, 1, VECTOR)
+        empty_recurrent_weights(0, 1, SCALAR)
+        quantise_input_weights(0, 0, [0, 1])
+        fh_grouped[2] = flip_rows(fh_raw[2], 2, [SCALAR])
+        quantise(fh_codes, fh_scales, 2 * BATCH, fh_grouped[2])
         open_recurrent_group(0, 0)
         for e in range(2):
             add_recurrent_pass(0, 0, e)
         empty_recurrent_group(0, 0, VECTOR)
+        quantise_features(1)
 
         last = AGENTS - 1
         for step in range(2 * AGENTS - 1):

import concourse.mybir as mybir
from concourse.masks import make_identity

F32 = mybir.dt.float32
BF16 = mybir.dt.bfloat16
U32 = mybir.dt.uint32
U8 = mybir.dt.uint8
FP8X4 = mybir.dt.float8_e4m3fn_x4
FUNC = mybir.ActivationFunctionType
ALU = mybir.AluOpType

P = 128
AGENTS = 8
BATCH = 128
M1 = 512
F = 1024
H = 256
G = 4 * H
BANK = 512
PASS_WORDS = 256

BIAS_BY_TRANSPOSE = 2


FLOPS = 2 * BATCH * AGENTS * (M1 * F + F * G + H * G)


def tile_ppo_actor_pa_kernel(tc, f_hid, h0, c0, W2, b2, W_ih, W_hh, b_ih, b_hh, out_0, out_1):
    nc = tc.nc
    with (
        tc.tile_pool(name="keep", bufs=1) as keep,
        tc.tile_pool(name="raw_hh", bufs=3) as raw_hh,
        tc.tile_pool(name="raw_ih", bufs=6) as raw_ih,
        tc.tile_pool(name="stage", bufs=2) as stage,
        tc.tile_pool(name="units", bufs=3) as units,
        tc.tile_pool(name="work", bufs=2) as work,
        tc.psum_pool(name="banks", bufs=8) as banks,
        tc.manual_schedule(),
    ):
        identity = keep.tile([P, P], F32)
        make_identity(nc, identity[:])

        warm = keep.tile([P, 2], F32)
        nc.vector.memset(warm[:], 0.0)
        nc.scalar.activation(out=warm[:, 1:2], in_=warm[:, 0:1], func=FUNC.Sigmoid)

        whh_raw = {}
        wih_raw = {}

        def load_input_weights(n, half):
            rows = W_ih[n, half * BANK : (half + 1) * BANK, :]
            wih_raw[(n, half)] = raw_ih.tile([P, 2, 2 * F], BF16, name="wih_raw")
            nc.sync.dma_start(out=wih_raw[(n, half)][:], in_=rows.rearrange("(q p j) k -> p q (j k)", p=P, j=2))

        def load_recurrent_weights(n):
            whh_raw[n] = raw_hh.tile([P, 4, 2 * H], BF16, name="whh_raw")
            nc.sync.dma_start(out=whh_raw[n][:], in_=W_hh[n].rearrange("(q p j) k -> p q (j k)", p=P, j=2))

        fh_raw = {first: keep.tile([P, 2, M1], BF16, name="fh_raw%d" % first) for first in range(0, AGENTS, 2)}
        w2_raw = [keep.tile([P, 4, M1], BF16, name="w2_raw%d" % c) for c in range(2)]
        vec_rows = keep.tile([P, 2 * P], BF16)
        nc.vector.memset(vec_rows[:].bitcast(F32), 0.0)
        b2_rows = keep.tile([P, 4 * P], BF16)
        nc.vector.memset(b2_rows[:].bitcast(F32), 0.0)
        h0_raw = keep.tile([P, AGENTS, H], BF16)
        c0_sb = keep.tile([P, AGENTS, H], BF16)

        bias_rows = keep.tile([P, (AGENTS - BIAS_BY_TRANSPOSE) * G], BF16)
        nc.gpsimd.memset(bias_rows[:].bitcast(F32), 0.0)
        ones = keep.tile([P, P], BF16)
        nc.gpsimd.memset(ones[:], 1.0)

        def load_f_hid(first):
            nc.sync.dma_start(out=fh_raw[first][:], in_=f_hid[:, first : first + 2, :])

        def load_state(tile, state, first):
            agents = slice(first, first + 4)
            nc.sync.dma_start(out=tile[:, agents, :], in_=state[agents].rearrange("n b k -> b n k"))

        def load_feature_weights(c):
            nc.sync.dma_start(out=w2_raw[c][:], in_=W2[c * BANK : (c + 1) * BANK, :].rearrange("(p t) k -> p t k", t=4))

        load_f_hid(0)
        load_feature_weights(0)
        nc.sync.dma_start(out=b2_rows[0:2, :], in_=b2.rearrange("(c w) -> c w", w=4 * P))
        nc.sync.dma_start(out=vec_rows[0:32, :], in_=b_ih.rearrange("n (q w) -> (n q) w", w=2 * P))
        nc.sync.dma_start(out=vec_rows[32:64, :], in_=b_hh.rearrange("n (q w) -> (n q) w", w=2 * P))
        load_feature_weights(1)
        load_input_weights(0, 0)
        load_state(h0_raw, h0, 0)
        load_recurrent_weights(0)
        load_input_weights(0, 1)
        load_f_hid(2)
        load_recurrent_weights(1)
        load_input_weights(1, 0)
        load_state(c0_sb, c0, 0)
        for row, bias in ((0, b_ih), (1, b_hh)):
            nc.sync.dma_start(
                out=bias_rows[row : row + 1, :], in_=bias[BIAS_BY_TRANSPOSE:AGENTS, :].rearrange("(o n) g -> o (n g)", o=1)
            )
        load_input_weights(1, 1)
        load_recurrent_weights(2)
        load_f_hid(4)
        load_f_hid(6)
        load_state(h0_raw, h0, 4)
        load_input_weights(2, 0)
        load_input_weights(2, 1)
        load_state(c0_sb, c0, 4)

        def flip_bank(words, word, grouped_words, copy_out):
            bank = banks.tile([P, BANK], F32, name="bank")
            for a in range(2):
                for u in range(2):
                    nc.tensor.transpose(
                        bank[:, (2 * a + u) * P : (2 * a + u + 1) * P],
                        words[:, a, word + u : word + PASS_WORDS : 2],
                        identity[:],
                    )
            copy_out(
                out=grouped_words.rearrange("p (a c u) -> p a c u", a=2, u=2),
                in_=bank[:].rearrange("p (a u c) -> p a c u", a=2, u=2),
            )

        def flip_blocks(bank, words, blocks):
            for i in blocks:
                nc.tensor.transpose(bank[:, i * P : (i + 1) * P], words[:, i * P : (i + 1) * P], identity[:])

        def flip_pairs(words, pairs, copy_out):
            bank = banks.tile([P, BANK], F32, name="bank")
            flip_blocks(bank, words, range(4))
            copy_out(out=pairs.rearrange("p c e -> p (c e)").bitcast(F32), in_=bank[:])

        SCALAR, VECTOR = nc.scalar.copy, nc.vector.tensor_copy

        fh_codes = keep.tile([P, AGENTS * BATCH], U32, align_bytes=64)
        fh_scales = keep.tile([P, AGENTS * BATCH], U8, align_bytes=64)
        w2_codes = keep.tile([P, F], U32, align_bytes=64)
        w2_scales = keep.tile([P, F], U8, align_bytes=64)

        def blocks_of_words(raw, count):
            return raw[:].rearrange("p n k -> p (n k)").bitcast(F32).rearrange("p (s w) -> p s w", s=count)

        def quantise(codes, scales, first, grouped):
            cols = slice(first, first + grouped.shape[1] // 4)
            nc.vector.quantize_mx(out=codes[:, cols].bitcast(FP8X4), scales=scales[:, cols], in_=grouped)

        def flip_rows(raw, count, copy_outs):
            grouped = stage.tile([P, count * 4 * P], BF16, name="grouped_rows", align_bytes=64)
            grouped_words = grouped[:].bitcast(F32)
            words = blocks_of_words(raw, count)
            for i in range(count // 2):
                cols = slice(i * BANK, (i + 1) * BANK)
                flip_bank(words[:, 2 * i : 2 * i + 2, :], 0, grouped_words[:, cols], copy_outs[i])
            return grouped[:]

        fh_grouped = {0: flip_rows(fh_raw[0], 2, [SCALAR])}
        w2_grouped = [flip_rows(w2_raw[0], 4, [SCALAR, SCALAR])]
        quantise(fh_codes, fh_scales, 0, fh_grouped[0])
        w2_grouped.append(flip_rows(w2_raw[1], 4, [SCALAR, VECTOR]))
        quantise(w2_codes, w2_scales, 0, w2_grouped[0])

        vec_bank = banks.tile([P, BANK], F32, name="bank")
        nc.tensor.transpose(vec_bank[:, 0:P], vec_rows[:].bitcast(F32), identity[:])
        for u in range(2):
            nc.tensor.transpose(
                vec_bank[:, (1 + u) * P : (2 + u) * P], b2_rows[:].bitcast(F32)[:, u : 2 * P : 2], identity[:]
            )
        b2_cols = keep.tile([P, 8], F32)
        for u in range(2):
            nc.vector.tensor_copy(
                out=b2_cols[:].rearrange("p (c u e) -> p c u e", u=2, e=2)[:, :, u, :],
                in_=vec_bank[:].bitcast(BF16)[:, 2 * (1 + u) * P : 2 * (1 + u) * P + 4].rearrange("p (c e) -> p c e", e=2),
            )
        vec_cols = keep.tile([P, 128], F32)
        nc.vector.tensor_copy(out=vec_cols[:], in_=vec_bank[:].bitcast(BF16)[:, 0:128])
        quantise(w2_codes, w2_scales, BANK, w2_grouped[1])
        gate_bias = keep.tile([P, 64], F32)
        nc.vector.tensor_tensor(out=gate_bias[:], in0=vec_cols[:, 0:64], in1=vec_cols[:, 64:128], op=ALU.add)

        feat_banks = {}
        feat_sums = {}
        feat_codes = {}
        feat_scales = {}

        def make_features(n, c):
            f_bank = banks.tile([P, BANK], F32, name="bank")
            cols = slice(n * BATCH, (n + 1) * BATCH)
            for t in range(4):
                s = 4 * c + t
                nc.tensor.matmul_mx(
                    out=f_bank[:, t * BATCH : (t + 1) * BATCH],
                    lhsT=w2_codes[:, s * P : (s + 1) * P].bitcast(FP8X4),
                    lhsT_scale=w2_scales[:, s * P : (s + 1) * P],
                    rhs=fh_codes[:, cols].bitcast(FP8X4),
                    rhs_scale=fh_scales[:, cols],
                    start=True,
                    stop=True,
                )
            feat_banks[(n, c)] = f_bank

        def add_feature_bias(n, c):
            if c == 0:
                feat_sums[n] = stage.tile([P, 2, BATCH, 4], BF16, name="feat_sums", align_bytes=64)
            nc.vector.tensor_tensor(
                out=feat_sums[n][:, c, :, :],
                in0=feat_banks[(n, c)][:].rearrange("p (t b) -> p b t", t=4),
                in1=b2_cols[:, 4 * c : 4 * c + 4].unsqueeze(1).broadcast_to([P, BATCH, 4]),
                op=ALU.add,
            )

        def rectify_features(n):
            values = feat_sums[n][:].rearrange("p c b t -> p (c b t)")
            nc.vector.tensor_scalar_max(out=values, in0=values, scalar1=0.0)

        def quantise_features(n):
            feat_codes[n] = units.tile([P, 2 * BATCH], U32, name="feat_codes", align_bytes=64)
            feat_scales[n] = units.tile([P, 2 * BATCH], U8, name="feat_scales", align_bytes=64)
            quantise(feat_codes[n], feat_scales[n], 0, feat_sums[n][:].rearrange("p c b t -> p (c b t)"))

        wih_grouped = {}
        wih_codes = {}
        wih_scales = {}
        whh_banks = {}
        whhT = {}
        hh_sb = {}
        mx_banks = {}
        gates = {}
        squashed = {}
        h_c = {}

        def code_block(n, half, gate, c):
            return 2 * gate + c if (n, half) == (AGENTS - 1, 1) else 2 * c + gate

        def flip_input_weights(n, half, gate):
            if gate == 0:
                wih_grouped[(n, half)] = stage.tile([P, 8 * BANK], BF16, name="wih_grouped", align_bytes=64)
            words = blocks_of_words(wih_raw[(n, half)], 4)
            grouped_words = wih_grouped[(n, half)][:].bitcast(F32)
            for c in range(2):
                i = code_block(n, half, gate, c)
                cols = slice(i * BANK, (i + 1) * BANK)
                flip_bank(words[:, 2 * gate : 2 * gate + 2, :], c * PASS_WORDS, grouped_words[:, cols], SCALAR)

        def quantise_input_weights(n, half, which):
            if which[0] == 0:
                wih_codes[(n, half)] = units.tile([P, 2 * BANK], U32, name="wih_codes", align_bytes=64)
                wih_scales[(n, half)] = units.tile([P, 2 * BANK], U8, name="wih_scales", align_bytes=64)
            values = slice(which[0] * 4 * BANK, (which[-1] + 1) * 4 * BANK)
            quantise(wih_codes[(n, half)], wih_scales[(n, half)], which[0] * BANK, wih_grouped[(n, half)][:, values])

        def flip_recurrent_weights(n, half, blocks):
            if (n, half) not in whh_banks:
                whh_banks[(n, half)] = banks.tile([P, BANK], F32, name="bank")
            words = whh_raw[n][:].rearrange("p q k -> p (q k)").bitcast(F32)
            flip_blocks(whh_banks[(n, half)], words[:, half * BANK : (half + 1) * BANK], blocks)

        def empty_recurrent_weights(n, half, copy_out):
            if n not in whhT:
                whhT[n] = work.tile([P, G, 2], BF16, name="whhT")
            pairs = whhT[n][:, half * BANK : (half + 1) * BANK, :]
            copy_out(out=pairs.rearrange("p c e -> p (c e)").bitcast(F32), in_=whh_banks[(n, half)][:])

        hh_banks = {}

        def open_recurrent_group(n, half):
            hh_bank = banks.tile([P, BANK], F32, name="bank")
            hh_banks[(n, half)] = hh_bank
            if n < BIAS_BY_TRANSPOSE:
                for i in range(4):
                    m = 8 * n + 4 * half + i
                    nc.tensor.matmul(
                        out=hh_bank[:, i * P : (i + 1) * P],
                        lhsT=gate_bias[:, m : m + 1].to_broadcast([P, P]),
                        rhs=identity[:],
                        is_transpose=True,
                        start=(i == 0),
                        stop=False,
                    )
            else:
                first = (n - BIAS_BY_TRANSPOSE) * G + half * BANK
                nc.tensor.matmul(
                    out=hh_bank[:],
                    lhsT=ones[:],
                    rhs=bias_rows[:, first : first + BANK].rearrange("k (q p j) -> k q j p", q=2, j=2),
                    start=True,
                    stop=False,
                )
        def add_recurrent_pass(n, half, e):
            nc.tensor.matmul(
                out=hh_banks[(n, half)][:],
                lhsT=h0T[:, n * BATCH : (n + 1) * BATCH, e],
                rhs=whhT[n][:, half * BANK : (half + 1) * BANK, e],
                start=False,
                stop=(e == 1),
            )

        def empty_recurrent_group(n, half, copy_out):
            hh_sb[(n, half)] = work.tile([P, BANK], F32, name="hh_sb")
            copy_out(
                out=hh_sb[(n, half)][:].rearrange("b (q p j) -> b q p j", q=2, j=2),
                in_=hh_banks[(n, half)][:].rearrange("b (q j p) -> b q p j", q=2, j=2),
            )

        def input_group(n, half, which):
            mx_bank = banks.tile([P, BANK], F32, name="bank")
            mx_banks[(n, half, which[0])] = mx_bank
            width = len(which) * H
            for c in range(2):
                block = code_block(n, half, which[0], c)
                cols = slice(block * H, block * H + width)
                nc.tensor.matmul_mx(
                    out=mx_bank[:, 0:width],
                    lhsT=feat_codes[n][:, c * BATCH : (c + 1) * BATCH].bitcast(FP8X4),
                    lhsT_scale=feat_scales[n][:, c * BATCH : (c + 1) * BATCH],
                    rhs=wih_codes[(n, half)][:, cols].bitcast(FP8X4),
                    rhs_scale=wih_scales[(n, half)][:, cols],
                    start=(c == 0),
                    stop=(c == 1),
                )

        def add_groups(n, half, which):
            width = len(which) * H
            mx_bank = mx_banks[(n, half, which[0])]
            if n not in gates:
                gates[n] = work.tile([P, G], F32, name="gates")
            first = which[0] * H
            nc.vector.tensor_tensor(
                out=gates[n][:, half * BANK + first : half * BANK + first + width].rearrange("b (q p j) -> b q p j", p=P, j=2),
                in0=mx_bank[:, 0:width].rearrange("b (q j p) -> b q p j", p=P, j=2),
                in1=hh_sb[(n, half)][:, first : first + width].rearrange("b (q p j) -> b q p j", p=P, j=2),
                op=ALU.add,
            )

        def squash_input_and_forget(n):
            squashed[n] = work.tile([P, G], F32, name="squashed")
            nc.scalar.activation(out=squashed[n][:, 0 : 2 * H], in_=gates[n][:, 0 : 2 * H], func=FUNC.Sigmoid)
            h_c[n] = work.tile([P, 2, H], F32, name="h_c")

        def keep_old_state(n):
            nc.vector.tensor_tensor(out=h_c[n][:, 0, :], in0=squashed[n][:, H : 2 * H], in1=c0_sb[:, n, :], op=ALU.mult)

        def squash_candidate(n):
            nc.scalar.activation(out=squashed[n][:, 2 * H : 3 * H], in_=gates[n][:, 2 * H : 3 * H], func=FUNC.Tanh)

        def squash_output_gate(n):
            nc.scalar.activation(out=squashed[n][:, 3 * H : 4 * H], in_=gates[n][:, 3 * H : 4 * H], func=FUNC.Sigmoid)

        def new_state(n):
            fresh = work.tile([P, H], F32, name="fresh")
            nc.vector.tensor_tensor(out=fresh[:], in0=squashed[n][:, 0:H], in1=squashed[n][:, 2 * H : 3 * H], op=ALU.mult)
            nc.vector.tensor_tensor(out=h_c[n][:, 1, :], in0=h_c[n][:, 0, :], in1=fresh[:], op=ALU.add)
            nc.sync.dma_start(out=out_1[n], in_=h_c[n][:, 1, :])

        tanh_c = {}

        def squash_state(n):
            tanh_c[n] = work.tile([P, H], F32, name="tanh_c")
            nc.scalar.activation(out=tanh_c[n][:], in_=h_c[n][:, 1, :], func=FUNC.Tanh)

        def new_output(n):
            nc.vector.tensor_tensor(out=h_c[n][:, 0, :], in0=squashed[n][:, 3 * H : 4 * H], in1=tanh_c[n][:], op=ALU.mult)
            nc.sync.dma_start(out=out_0[n], in_=h_c[n][:, 0, :])

        flip_input_weights(0, 0, 0)
        for n in range(2):
            for c in range(2):
                make_features(n, c)
        for n in range(2):
            for c in range(2):
                add_feature_bias(n, c)
            rectify_features(n)
        flip_input_weights(0, 0, 1)
        h0T = keep.tile([P, AGENTS * BATCH, 2], BF16)
        h0_words = h0_raw[:].rearrange("p n k -> p (n k)").bitcast(F32)
        flip_pairs(h0_words[:, 0:BANK], h0T[:, 0:BANK, :], SCALAR)
        flip_recurrent_weights(0, 0, range(4))
        empty_recurrent_weights(0, 0, SCALAR)
        quantise_features(0)
        flip_recurrent_weights(0, 1, range(4))
        empty_recurrent_weights(0, 1, SCALAR)
        quantise_input_weights(0, 0, [0, 1])
        fh_grouped[2] = flip_rows(fh_raw[2], 2, [SCALAR])
        quantise(fh_codes, fh_scales, 2 * BATCH, fh_grouped[2])
        open_recurrent_group(0, 0)
        for e in range(2):
            add_recurrent_pass(0, 0, e)
        empty_recurrent_group(0, 0, VECTOR)
        quantise_features(1)

        last = AGENTS - 1
        for step in range(2 * AGENTS - 1):
            n, half = divmod(step, 2)
            m, mhalf = divmod(step + 1, 2)
            flip_input_weights(m, mhalf, 0)
            if n < last:
                flip_recurrent_weights(n + 1, half, range(2))
            if half == 0 and n + 3 < AGENTS:
                load_input_weights(n + 3, 0)
                load_recurrent_weights(n + 3)
            if half == 1:
                if n > 0:
                    new_state(n - 1)
                squash_input_and_forget(n)
            else:
                if n > 1:
                    new_output(n - 2)
                if n > 0:
                    keep_old_state(n - 1)
                    squash_candidate(n - 1)
                    squash_output_gate(n - 1)
            if half == 0 and 0 < n < last:
                rectify_features(n + 1)
            if n in (1, 3) and half == 1:
                quantise(fh_codes, fh_scales, (n + 3) * BATCH, fh_grouped[n + 3])
            open_recurrent_group(m, mhalf)
            if n == last:
                quantise_input_weights(last, 1, [0])
            flip_input_weights(m, mhalf, 1)
            if half == 0 and n + 3 < AGENTS:
                load_input_weights(n + 3, 1)
            if n in (1, 3) and half == 0:
                fh_grouped[n + 3] = flip_rows(fh_raw[n + 3], 2, [SCALAR])
            if step == 4:
                flip_pairs(h0_words[:, BANK : 2 * BANK], h0T[:, BANK : 2 * BANK, :], VECTOR)
            if n < last:
                flip_recurrent_weights(n + 1, half, range(2, 4))
                empty_recurrent_weights(n + 1, half, VECTOR if half else SCALAR)
            if half == 1 and n > 0:
                squash_state(n - 1)
            if half == 0 and 0 < n < last:
                quantise_features(n + 1)
            add_recurrent_pass(m, mhalf, 0)
            input_group(n, half, [0, 1])
            if n + 2 < AGENTS:
                make_features(n + 2, half)
            add_recurrent_pass(m, mhalf, 1)
            add_groups(n, half, [0, 1])
            empty_recurrent_group(m, mhalf, SCALAR)
            quantise_input_weights(m, mhalf, [1] if n == last else [0, 1])
            if n + 2 < AGENTS:
                add_feature_bias(n + 2, half)

        squash_input_and_forget(last)
        input_group(last, 1, [0])
        add_groups(last, 1, [0])
        squash_candidate(last)
        new_state(last - 1)
        squash_state(last - 1)
        keep_old_state(last)
        new_state(last)
        input_group(last, 1, [1])
        add_groups(last, 1, [1])
        squash_state(last)
        squash_output_gate(last)
        new_output(last - 1)
        new_output(last)
